import numpy as np
import ml_dtypes


def mxq(x, axis, fmt="e4m3"):
    dtype, down = {"e4m3": (ml_dtypes.float8_e4m3fn, 7), "e5m2": (ml_dtypes.float8_e5m2, 14)}[fmt]
    v = np.moveaxis(np.asarray(x, np.float32).astype(ml_dtypes.bfloat16).astype(np.float64), axis, -1)
    blocks = v.reshape(v.shape[:-1] + (-1, 32))
    amax = np.abs(blocks).max(-1, keepdims=True)
    byte = np.maximum(np.where(amax > 0, np.frexp(amax)[1] - 1 + 127, 0) - down, 1)
    scale = np.exp2(byte - 127.0)
    codes = (blocks / scale).astype(np.float32).astype(dtype).astype(np.float64)
    return np.moveaxis((codes * scale).reshape(v.shape), -1, axis)


WIDE = False


def mx_kscale(k):
    if not WIDE:
        return np.ones(k)
    levels = np.array([10, -10, 5, -5, 0])
    if k % 512:
        return np.exp2(np.random.permutation(np.resize(levels, k // 32))).repeat(32)
    a = np.empty((k // 512, 16))
    for p in range(k // 512):
        a[p, :8] = np.random.permutation(np.resize(levels, 8))
        for g in range(8):
            far = levels[np.abs(levels - a[p, g]) >= 10]
            a[p, g + 8] = far[np.random.randint(len(far))]
    return np.exp2(a.ravel()).repeat(32)


BF16 = ml_dtypes.bfloat16


def bf(x):
    return np.asarray(x, np.float32).astype(BF16)


def f64(x):
    return np.asarray(x).astype(np.float64)


B, D, H = 512, 1024, 1024
QH = True


def sigmoid(v):
    return 1.0 / (1.0 + np.exp(-v))


def xavier(rows, cols):
    limit = np.sqrt(6.0 / (rows + cols))
    return np.random.uniform(-limit, limit, (rows, cols))


def setup_inputs():
    s = mx_kscale(D)
    t = mx_kscale(H) if QH else np.ones(H)
    inp = {"x": bf(np.random.standard_normal((B, D)) * s), "h0": bf(np.random.standard_normal((B, H)) * t), "c0": bf(np.random.standard_normal((B, H)))}
    for n in ("i", "f", "g", "o"):
        inp["W_i" + n] = bf(xavier(H, D) / s)
        inp["b_i" + n] = bf(np.random.standard_normal(H) * 0.1)
        inp["W_h" + n] = bf(xavier(H, H) / t)
        inp["b_h" + n] = bf(np.random.standard_normal(H) * 0.1)
    return inp


def reference(x, h0, c0,
              W_ii, b_ii, W_hi, b_hi,
              W_if, b_if, W_hf, b_hf,
              W_ig, b_ig, W_hg, b_hg,
              W_io, b_io, W_ho, b_ho):
    Wx = np.concatenate([f64(W_ii), f64(W_if), f64(W_ig), f64(W_io)], axis=0)
    Wh = np.concatenate([f64(W_hi), f64(W_hf), f64(W_hg), f64(W_ho)], axis=0)
    b = np.concatenate([f64(b_ii) + f64(b_hi), f64(b_if) + f64(b_hf), f64(b_ig) + f64(b_hg), f64(b_io) + f64(b_ho)])
    gx = mxq(f64(x), 1, "e4m3") @ mxq(Wx, 1, "e4m3").T
    if QH:
        gh = mxq(f64(h0), 1, "e4m3") @ mxq(Wh, 1, "e4m3").T
    else:
        gh = f64(h0) @ Wh.T
    gates = gx + gh + b
    i_t = sigmoid(gates[:, 0 * H:1 * H])
    f_t = sigmoid(gates[:, 1 * H:2 * H])
    g_t = np.tanh(gates[:, 2 * H:3 * H])
    o_t = sigmoid(gates[:, 3 * H:4 * H])
    c_t = f_t * c0_f(c0) + i_t * g_t
    h_t = o_t * np.tanh(c_t)
    return (h_t, c_t)


def c0_f(c0):
    return f64(c0)

@@ -1,0 +1,295 @@
+from contextlib import ExitStack
+
+import concourse.mybir as mybir
+from concourse.masks import make_identity
+
+F32 = mybir.dt.float32
+BF16 = mybir.dt.bfloat16
+U32 = mybir.dt.uint32
+U8 = mybir.dt.uint8
+FP8X4 = mybir.dt.float8_e4m3fn_x4
+ACT = mybir.ActivationFunctionType
+ALU = mybir.AluOpType
+
+P = 128
+BATCH = 512
+K = 1024
+HID = 1024
+NT = HID // P
+NR = 2 * NT
+FLOPS = 2 * BATCH * (2 * K) * (4 * HID)
+
+AHEAD = 10
+C0_AFTER = 3
+STORE_GROUPS = ((0, 1), (2, 3), (4, 5), (6,), (7,))
+W_EVAC_ON_SCALAR = (True, False, True, True)
+TAIL_PARTS = 2
+
+
+def tile_lstmcell_kernel(
+    tc, x, h0, c0,
+    W_ii, b_ii, W_hi, b_hi,
+    W_if, b_if, W_hf, b_hf,
+    W_ig, b_ig, W_hg, b_hg,
+    W_io, b_io, W_ho, b_ho,
+    out_0, out_1,
+):
+    nc = tc.nc
+    weights = ((W_ii, W_hi), (W_ig, W_hg), (W_if, W_hf), (W_io, W_ho))
+    biases = ((b_ii, b_hi), (b_ig, b_hg), (b_if, b_hf), (b_io, b_ho))
+    funcs = (ACT.Sigmoid, ACT.Tanh, ACT.Sigmoid, ACT.Sigmoid)
+    out_h = out_0.rearrange("(p t) h -> p t h", t=4)
+    out_c = out_1.rearrange("(p t) h -> p t h", t=4)
+
+    with ExitStack() as ctx:
+        const = ctx.enter_context(tc.tile_pool(name="const", bufs=1))
+        wraw_pool = ctx.enter_context(tc.tile_pool(name="wraw", bufs=4 * AHEAD))
+        grp_pool = ctx.enter_context(tc.tile_pool(name="grp", bufs=3))
+        code_pool = ctx.enter_context(tc.tile_pool(name="code", bufs=3))
+        act_pool = ctx.enter_context(tc.tile_pool(name="act", bufs=2))
+        ep_pool = ctx.enter_context(tc.tile_pool(name="ep", bufs=2))
+        out_pool = ctx.enter_context(tc.tile_pool(name="outp", bufs=2))
+        acc_pool = ctx.enter_context(tc.psum_pool(name="acc", bufs=2))
+        tr_pool = ctx.enter_context(tc.psum_pool(name="tr", bufs=6))
+        ctx.enter_context(tc.manual_schedule())
+
+        ident = const.tile([P, P], F32, name="ident")
+        make_identity(nc, ident[:])
+        warm = const.tile([P, 1], F32, name="warm")
+        nc.vector.memset(warm[:], 0.0)
+        braw = const.tile([P, 2 * P], BF16, name="braw")
+        nc.vector.memset(braw[:], 0.0)
+
+        zeros = const.tile([P, 512], BF16, name="zeros")
+        nc.vector.memset(zeros[:], 0.0)
+
+        def keep_clock(n, name):
+            idle = acc_pool.tile([P, 512], F32, name=name, tag="acc")
+            for i in range(n):
+                nc.tensor.matmul(out=idle[:], lhsT=zeros[:, 0:P], rhs=zeros[:], start=True, stop=True)
+
+        keep_clock(10, "idle_start")
+
+        xraw = []
+        for s, src in enumerate((x, h0)):
+            xr = const.tile([P, 4 * K], BF16, name="xraw%d" % s)
+            view = src.rearrange("(p t) k -> p t k", t=4)
+            for th in range(2):
+                nc.sync.dma_start(
+                    out=xr[:, th * 2 * K:(th + 1) * 2 * K].rearrange("p (t k) -> p t k", t=2),
+                    in_=view[:, 2 * th:2 * th + 2, :],
+                )
+            xraw.append(xr)
+        for q in range(4):
+            for s in range(2):
+                nc.scalar.dma_start(
+                    out=braw[8 * q:8 * q + 8, s * P:(s + 1) * P],
+                    in_=biases[q][s].rearrange("(j p) -> j p", p=P),
+                )
+        nc.scalar.activation(out=warm[:], in_=warm[:], func=ACT.Sigmoid)
+
+        c0_sb = const.tile([P, 4 * HID], BF16, name="c0_sb")
+        c0_v = c0_sb[:].rearrange("p (t h) -> p t h", t=4)
+        wraw = {}
+
+        def load_round(r):
+            j = r // 2
+            tiles = []
+            for hh in range(2):
+                for s in range(2):
+                    w = wraw_pool.tile([P, K], BF16, name="w%d_%d_%d" % (r, hh, s), tag="w")
+                    nc.sync.dma_start(out=w[:], in_=weights[2 * (r % 2) + hh][s][j * P:(j + 1) * P, :])
+                    tiles.append(w)
+            wraw[r] = tiles
+            if r == C0_AFTER:
+                nc.sync.dma_start(out=c0_sb[:], in_=c0.rearrange("(p t) h -> p (t h)", t=4))
+
+        for r in range(AHEAD):
+            load_round(r)
+
+        def transpose_bank(src32, cols, dst32, on_scalar, name):
+            bank = tr_pool.tile([P, 512], F32, name=name, tag="tr")
+            for i, c in enumerate(cols):
+                nc.tensor.transpose(bank[:, i * P:(i + 1) * P], src32[:, c:c + 2 * P - 1:2], ident[:])
+            src = bank[:].rearrange("p (a u c) -> p a c u", a=2, u=2)
+            dst = dst32.rearrange("p (a c u) -> p a c u", a=2, u=2)
+            if on_scalar:
+                nc.scalar.copy(out=dst, in_=src)
+            else:
+                nc.vector.tensor_copy(out=dst, in_=src)
+
+        xq = const.tile([P, 4 * 512], U32, name="xq", align_bytes=64)
+        xs = const.tile([P, 4 * 512], U8, name="xs", align_bytes=64)
+        xgrp = []
+        for s in range(2):
+            xg = grp_pool.tile([P, 4096], BF16, name="xgrp%d" % s, tag="grp", align_bytes=64)
+            xgrp.append(xg)
+
+        def tr_x(s, th):
+            x32 = xraw[s][:].bitcast(F32)
+            g32 = xgrp[s][:].bitcast(F32)
+            for g in range(2):
+                cols = [(2 * th + tt) * 512 + 256 * g + u for tt in range(2) for u in range(2)]
+                base = g * 1024 + th * 512
+                transpose_bank(x32, cols, g32[:, base:base + 512], g == 0, "xb%d%d%d" % (s, th, g))
+
+        def quant_x(s):
+            nc.vector.quantize_mx(
+                out=xq[:, s * 1024:(s + 1) * 1024].bitcast(FP8X4),
+                scales=xs[:, s * 1024:(s + 1) * 1024],
+                in_=xgrp[s][:],
+            )
+
+        grp = {}
+        wq = {}
+        ws = {}
+        gate = {}
+        prod = {}
+        banks = {}
+        outs = {}
+        tanh_c = {}
+
+        def tr_w(r):
+            grp[r] = grp_pool.tile([P, 4096], BF16, name="grp%d" % r, tag="grp", align_bytes=64)
+            g32 = grp[r][:].bitcast(F32)
+            for m in range(4):
+                transpose_bank(
+                    wraw[r][m][:].bitcast(F32), (0, 1, 256, 257), g32[:, m * 512:(m + 1) * 512],
+                    W_EVAC_ON_SCALAR[m], "wb%d_%d" % (r, m),
+                )
+            if r + AHEAD < NR:
+                load_round(r + AHEAD)
+
+        def quant(r):
+            wq[r] = code_pool.tile([P, 1024], U32, name="wq%d" % r, tag="wq", align_bytes=64)
+            ws[r] = code_pool.tile([P, 1024], U8, name="ws%d" % r, tag="ws", align_bytes=64)
+            for hh in range(2):
+                nc.vector.quantize_mx(
+                    out=wq[r][:, hh * 512:(hh + 1) * 512].bitcast(FP8X4),
+                    scales=ws[r][:, hh * 512:(hh + 1) * 512],
+                    in_=grp[r][:, hh * 2048:(hh + 1) * 2048],
+                )
+
+        def mx_act(r, hh):
+            j = r // 2
+            q = 2 * (r % 2) + hh
+            acc = acc_pool.tile([P, 512], F32, name="acc%d_%d" % (j, q), tag="acc")
+            for s in range(2):
+                for g in range(2):
+                    wc = (2 * hh + s) * 256 + g * 128
+                    xc = (2 * s + g) * 512
+                    nc.tensor.matmul_mx(
+                        out=acc[:],
+                        lhsT=wq[r][:, wc:wc + 128].bitcast(FP8X4),
+                        lhsT_scale=ws[r][:, wc:wc + 128],
+                        rhs=xq[:, xc:xc + 512].bitcast(FP8X4),
+                        rhs_scale=xs[:, xc:xc + 512],
+                        start=(s == 0 and g == 0),
+                        stop=(s == 1 and g == 1),
+                    )
+            a = act_pool.tile([P, 512], F32, name="gate%d_%d" % (j, q), tag="gate%d" % q)
+            nc.scalar.activation(
+                out=a[:], in_=acc[:], func=funcs[q],
+                bias=bias_sb[:, 8 * q + j:8 * q + j + 1], scale=1.0,
+            )
+            gate[(j, q)] = a
+
+        def mul_ig(j):
+            t = act_pool.tile([P, 512], F32, name="ig%d" % j, tag="ig")
+            nc.vector.tensor_tensor(out=t[:], in0=gate[(j, 0)][:], in1=gate[(j, 1)][:], op=ALU.mult)
+            prod[j] = t
+
+        def tr_out(j, key):
+            src = {"f": gate[(j, 2)], "u": prod[j], "o": gate[(j, 3)]}[key]
+            bank = tr_pool.tile([P, 512], F32, name="ob%s%d" % (key, j), tag="tr")
+            for t in range(4):
+                nc.tensor.transpose(bank[:, t * P:(t + 1) * P], src[:, t * P:(t + 1) * P], ident[:])
+            banks[(j, key)] = bank[:].rearrange("p (t h) -> p t h", t=4)
+
+        def group_of(j):
+            for grp_js in STORE_GROUPS:
+                if j in grp_js:
+                    return grp_js
+            return None
+
+        def ep_c(j, parts):
+            js = group_of(j)
+            width = P * len(js)
+            if j == js[0]:
+                outs[js] = (
+                    out_pool.tile([P, 4, width], F32, name="oh%d" % j, tag="oh"),
+                    out_pool.tile([P, 4, width], F32, name="oc%d" % j, tag="oc"),
+                )
+            off = (j - js[0]) * P
+            t1 = ep_pool.tile([P, 4, P], F32, name="t1_%d" % j, tag="t1")
+            th = ep_pool.tile([P, 4, P], F32, name="th%d" % j, tag="th")
+            n = 4 // parts
+            for part in range(parts):
+                ts = slice(part * n, (part + 1) * n)
+                oc_v = outs[js][1][:, ts, off:off + P]
+                nc.vector.tensor_tensor(
+                    out=t1[:, ts, :], in0=banks[(j, "f")][:, ts, :], in1=c0_v[:, ts, j * P:(j + 1) * P], op=ALU.mult,
+                )
+                nc.vector.tensor_tensor(out=oc_v, in0=banks[(j, "u")][:, ts, :], in1=t1[:, ts, :], op=ALU.add)
+                nc.scalar.activation(out=th[:, ts, :], in_=oc_v, func=ACT.Tanh)
+            tanh_c[j] = th
+            if j == js[-1]:
+                nc.sync.dma_start(out=out_c[:, :, js[0] * P:(js[-1] + 1) * P], in_=outs[js][1][:])
+
+        def ep_h(j, parts):
+            js = group_of(j)
+            off = (j - js[0]) * P
+            n = 4 // parts
+            for part in range(parts):
+                ts = slice(part * n, (part + 1) * n)
+                nc.vector.tensor_tensor(
+                    out=outs[js][0][:, ts, off:off + P], in0=banks[(j, "o")][:, ts, :], in1=tanh_c[j][:, ts, :],
+                    op=ALU.mult,
+                )
+                if j == js[-1]:
+                    nc.sync.dma_start(out=out_h[:, ts, js[0] * P:(js[-1] + 1) * P], in_=outs[js][0][:, ts, :])
+
+        tr_x(0, 0)
+        keep_clock(2, "idle_a")
+        tr_x(0, 1)
+        keep_clock(2, "idle_b")
+        tr_x(1, 0)
+        keep_clock(2, "idle_c")
+        quant_x(0)
+        tr_x(1, 1)
+        keep_clock(2, "idle_d")
+
+        bsum = const.tile([P, P], F32, name="bsum")
+        nc.vector.tensor_tensor(out=bsum[:], in0=braw[:, 0:P], in1=braw[:, P:2 * P], op=ALU.add)
+        pb = tr_pool.tile([P, 512], F32, name="pb", tag="tr")
+        nc.tensor.transpose(pb[:, 0:P], bsum[:], ident[:])
+        bias_sb = const.tile([P, 32], F32, name="bias_sb")
+        nc.vector.tensor_copy(out=bias_sb[:], in_=pb[:, 0:32])
+
+        tr_w(0)
+        keep_clock(2, "idle_e")
+        quant_x(1)
+        quant(0)
+        for r in range(NR):
+            m = r // 2
+            if r + 1 < NR:
+                tr_w(r + 1)
+            if r % 2 == 0:
+                if m >= 1:
+                    tr_out(m - 1, "f")
+                    tr_out(m - 1, "u")
+                    ep_c(m - 1, 1)
+            else:
+                if m >= 1:
+                    tr_out(m - 1, "o")
+                    ep_h(m - 1, 1)
+                mul_ig(m)
+            if r + 1 < NR:
+                quant(r + 1)
+            mx_act(r, 0)
+            mx_act(r, 1)
+        tr_out(NT - 1, "f")
+        tr_out(NT - 1, "u")
+        tr_out(NT - 1, "o")
+        ep_c(NT - 1, TAIL_PARTS)
+        ep_h(NT - 1, TAIL_PARTS)

@@ -22,7 +22,7 @@ FLOPS = 2 * BATCH * (2 * K) * (4 * HID)
 AHEAD = 10
 C0_AFTER = 3
 STORE_GROUPS = ((0, 1), (2, 3), (4, 5), (6,), (7,))
-W_EVAC_ON_SCALAR = (True, False, True, True)
+W_EVAC_ON_SCALAR = (True, True, True, True)
 TAIL_PARTS = 2
 
 
@@ -44,6 +44,7 @@ def tile_lstmcell_kernel(
     with ExitStack() as ctx:
         const = ctx.enter_context(tc.tile_pool(name="const", bufs=1))
         wraw_pool = ctx.enter_context(tc.tile_pool(name="wraw", bufs=4 * AHEAD))
+        wperm_pool = ctx.enter_context(tc.tile_pool(name="wperm", bufs=8))
         grp_pool = ctx.enter_context(tc.tile_pool(name="grp", bufs=3))
         code_pool = ctx.enter_context(tc.tile_pool(name="code", bufs=3))
         act_pool = ctx.enter_context(tc.tile_pool(name="act", bufs=2))
@@ -91,6 +92,7 @@ def tile_lstmcell_kernel(
         c0_sb = const.tile([P, 4 * HID], BF16, name="c0_sb")
         c0_v = c0_sb[:].rearrange("p (t h) -> p t h", t=4)
         wraw = {}
+        wperm = {}
 
         def load_round(r):
             j = r // 2
@@ -107,10 +109,10 @@ def tile_lstmcell_kernel(
         for r in range(AHEAD):
             load_round(r)
 
-        def transpose_bank(src32, cols, dst32, on_scalar, name):
+        def transpose_bank(src32, cols, step, dst32, on_scalar, name):
             bank = tr_pool.tile([P, 512], F32, name=name, tag="tr")
             for i, c in enumerate(cols):
-                nc.tensor.transpose(bank[:, i * P:(i + 1) * P], src32[:, c:c + 2 * P - 1:2], ident[:])
+                nc.tensor.transpose(bank[:, i * P:(i + 1) * P], src32[:, c:c + step * (P - 1) + 1:step], ident[:])
             src = bank[:].rearrange("p (a u c) -> p a c u", a=2, u=2)
             dst = dst32.rearrange("p (a c u) -> p a c u", a=2, u=2)
             if on_scalar:
@@ -131,7 +133,7 @@ def tile_lstmcell_kernel(
             for g in range(2):
                 cols = [(2 * th + tt) * 512 + 256 * g + u for tt in range(2) for u in range(2)]
                 base = g * 1024 + th * 512
-                transpose_bank(x32, cols, g32[:, base:base + 512], g == 0, "xb%d%d%d" % (s, th, g))
+                transpose_bank(x32, cols, 2, g32[:, base:base + 512], g == 0, "xb%d%d%d" % (s, th, g))
 
         def quant_x(s):
             nc.vector.quantize_mx(
@@ -149,17 +151,28 @@ def tile_lstmcell_kernel(
         outs = {}
         tanh_c = {}
 
+        def permute(r):
+            tiles = []
+            for m in range(4):
+                w = wperm_pool.tile([P, K], BF16, name="wp%d_%d" % (r, m), tag="wp")
+                nc.vector.tensor_copy(
+                    out=w[:].bitcast(F32).rearrange("p (g u q) -> p g u q", g=2, u=2),
+                    in_=wraw[r][m][:].bitcast(F32).rearrange("p (g q u) -> p g u q", g=2, u=2),
+                )
+                tiles.append(w)
+            wperm[r] = tiles
+            if r + AHEAD < NR:
+                load_round(r + AHEAD)
+
         def tr_w(r):
             grp[r] = grp_pool.tile([P, 4096], BF16, name="grp%d" % r, tag="grp", align_bytes=64)
             g32 = grp[r][:].bitcast(F32)
             for m in range(4):
+                src, cols, step = (wperm[r][m], (0, 128, 256, 384), 1) if r in wperm else (wraw[r][m], (0, 1, 256, 257), 2)
                 transpose_bank(
-                    wraw[r][m][:].bitcast(F32), (0, 1, 256, 257), g32[:, m * 512:(m + 1) * 512],
+                    src[:].bitcast(F32), cols, step, g32[:, m * 512:(m + 1) * 512],
                     W_EVAC_ON_SCALAR[m], "wb%d_%d" % (r, m),
                 )
-            if r + AHEAD < NR:
-                load_round(r + AHEAD)
-
         def quant(r):
             wq[r] = code_pool.tile([P, 1024], U32, name="wq%d" % r, tag="wq", align_bytes=64)
             ws[r] = code_pool.tile([P, 1024], U8, name="ws%d" % r, tag="ws", align_bytes=64)
@@ -270,8 +283,12 @@ def tile_lstmcell_kernel(
         keep_clock(2, "idle_e")
         quant_x(1)
         quant(0)
+        load_round(AHEAD)
+        permute(1)
         for r in range(NR):
             m = r // 2
+            if r + 2 < NR:
+                permute(r + 2)
             if r + 1 < NR:
                 tr_w(r + 1)
             if r % 2 == 0:

@@ -22,7 +22,6 @@ FLOPS = 2 * BATCH * (2 * K) * (4 * HID)
 AHEAD = 10
 C0_AFTER = 3
 STORE_GROUPS = ((0, 1), (2, 3), (4, 5), (6,), (7,))
-W_EVAC_ON_SCALAR = (True, True, True, True)
 TAIL_PARTS = 2
 
 
@@ -56,57 +55,60 @@ def tile_lstmcell_kernel(
 
         ident = const.tile([P, P], F32, name="ident")
         make_identity(nc, ident[:])
+        zeros = const.tile([P, 512], BF16, name="zeros")
+        nc.vector.memset(zeros[:], 0.0)
         warm = const.tile([P, 1], F32, name="warm")
         nc.vector.memset(warm[:], 0.0)
         braw = const.tile([P, 2 * P], BF16, name="braw")
         nc.vector.memset(braw[:], 0.0)
-
-        zeros = const.tile([P, 512], BF16, name="zeros")
-        nc.vector.memset(zeros[:], 0.0)
 
         def keep_clock(n, name):
             idle = acc_pool.tile([P, 512], F32, name=name, tag="acc")
             for i in range(n):
                 nc.tensor.matmul(out=idle[:], lhsT=zeros[:, 0:P], rhs=zeros[:], start=True, stop=True)
 
-        keep_clock(10, "idle_start")
+        keep_clock(6, "idle_start")
 
-        xraw = []
-        for s, src in enumerate((x, h0)):
-            xr = const.tile([P, 4 * K], BF16, name="xraw%d" % s)
-            view = src.rearrange("(p t) k -> p t k", t=4)
+        xraw = [const.tile([P, 4 * K], BF16, name="xraw%d" % s) for s in range(2)]
+
+        def load_x(s):
+            view = (x, h0)[s].rearrange("(p t) k -> p t k", t=4)
             for th in range(2):
                 nc.sync.dma_start(
-                    out=xr[:, th * 2 * K:(th + 1) * 2 * K].rearrange("p (t k) -> p t k", t=2),
+                    out=xraw[s][:, th * 2 * K:(th + 1) * 2 * K].rearrange("p (t k) -> p t k", t=2),
                     in_=view[:, 2 * th:2 * th + 2, :],
                 )
-            xraw.append(xr)
+
+        nc.scalar.activation(out=warm[:], in_=warm[:], func=ACT.Sigmoid)
         for q in range(4):
             for s in range(2):
                 nc.scalar.dma_start(
                     out=braw[8 * q:8 * q + 8, s * P:(s + 1) * P],
                     in_=biases[q][s].rearrange("(j p) -> j p", p=P),
                 )
-        nc.scalar.activation(out=warm[:], in_=warm[:], func=ACT.Sigmoid)
 
         c0_sb = const.tile([P, 4 * HID], BF16, name="c0_sb")
         c0_v = c0_sb[:].rearrange("p (t h) -> p t h", t=4)
         wraw = {}
         wperm = {}
 
-        def load_round(r):
+        def load_half(r, s):
             j = r // 2
-            tiles = []
             for hh in range(2):
-                for s in range(2):
-                    w = wraw_pool.tile([P, K], BF16, name="w%d_%d_%d" % (r, hh, s), tag="w")
-                    nc.sync.dma_start(out=w[:], in_=weights[2 * (r % 2) + hh][s][j * P:(j + 1) * P, :])
-                    tiles.append(w)
-            wraw[r] = tiles
+                w = wraw_pool.tile([P, K], BF16, name="w%d_%d_%d" % (r, s, hh), tag="w")
+                nc.sync.dma_start(out=w[:], in_=weights[2 * (r % 2) + hh][s][j * P:(j + 1) * P, :])
+                wraw[(r, s, hh)] = w
+
+        def load_round(r):
+            load_half(r, 0)
+            load_half(r, 1)
             if r == C0_AFTER:
                 nc.sync.dma_start(out=c0_sb[:], in_=c0.rearrange("(p t) h -> p (t h)", t=4))
 
-        for r in range(AHEAD):
+        for s in range(2):
+            load_x(s)
+            load_half(0, s)
+        for r in range(1, AHEAD):
             load_round(r)
 
         def transpose_bank(src32, cols, step, dst32, on_scalar, name):
@@ -136,15 +138,17 @@ def tile_lstmcell_kernel(
                 transpose_bank(x32, cols, 2, g32[:, base:base + 512], g == 0, "xb%d%d%d" % (s, th, g))
 
         def quant_x(s):
-            nc.vector.quantize_mx(
-                out=xq[:, s * 1024:(s + 1) * 1024].bitcast(FP8X4),
-                scales=xs[:, s * 1024:(s + 1) * 1024],
-                in_=xgrp[s][:],
-            )
+            for g in range(2):
+                c = (2 * s + g) * 512
+                nc.vector.quantize_mx(
+                    out=xq[:, c:c + 512].bitcast(FP8X4), scales=xs[:, c:c + 512],
+                    in_=xgrp[s][:, g * 2048:(g + 1) * 2048],
+                )
 
         grp = {}
         wq = {}
         ws = {}
+        accs = {}
         gate = {}
         prod = {}
         banks = {}
@@ -152,54 +156,60 @@ def tile_lstmcell_kernel(
         tanh_c = {}
 
         def permute(r):
-            tiles = []
-            for m in range(4):
-                w = wperm_pool.tile([P, K], BF16, name="wp%d_%d" % (r, m), tag="wp")
-                nc.vector.tensor_copy(
-                    out=w[:].bitcast(F32).rearrange("p (g u q) -> p g u q", g=2, u=2),
-                    in_=wraw[r][m][:].bitcast(F32).rearrange("p (g q u) -> p g u q", g=2, u=2),
-                )
-                tiles.append(w)
-            wperm[r] = tiles
+            for s in range(2):
+                for hh in range(2):
+                    w = wperm_pool.tile([P, K], BF16, name="wp%d_%d_%d" % (r, s, hh), tag="wp")
+                    nc.vector.tensor_copy(
+                        out=w[:].bitcast(F32).rearrange("p (g u q) -> p g u q", g=2, u=2),
+                        in_=wraw[(r, s, hh)][:].bitcast(F32).rearrange("p (g q u) -> p g u q", g=2, u=2),
+                    )
+                    wperm[(r, s, hh)] = w
             if r + AHEAD < NR:
                 load_round(r + AHEAD)
 
-        def tr_w(r):
-            grp[r] = grp_pool.tile([P, 4096], BF16, name="grp%d" % r, tag="grp", align_bytes=64)
+        def tr_w(r, s):
+            if s == 0:
+                grp[r] = grp_pool.tile([P, 4096], BF16, name="grp%d" % r, tag="grp", align_bytes=64)
             g32 = grp[r][:].bitcast(F32)
-            for m in range(4):
-                src, cols, step = (wperm[r][m], (0, 128, 256, 384), 1) if r in wperm else (wraw[r][m], (0, 1, 256, 257), 2)
-                transpose_bank(
-                    src[:].bitcast(F32), cols, step, g32[:, m * 512:(m + 1) * 512],
-                    W_EVAC_ON_SCALAR[m], "wb%d_%d" % (r, m),
-                )
-        def quant(r):
-            wq[r] = code_pool.tile([P, 1024], U32, name="wq%d" % r, tag="wq", align_bytes=64)
-            ws[r] = code_pool.tile([P, 1024], U8, name="ws%d" % r, tag="ws", align_bytes=64)
             for hh in range(2):
-                nc.vector.quantize_mx(
-                    out=wq[r][:, hh * 512:(hh + 1) * 512].bitcast(FP8X4),
-                    scales=ws[r][:, hh * 512:(hh + 1) * 512],
-                    in_=grp[r][:, hh * 2048:(hh + 1) * 2048],
+                key = (r, s, hh)
+                m = 2 * s + hh
+                src, cols, step = (wperm[key], (0, 128, 256, 384), 1) if key in wperm else (wraw[key], (0, 1, 256, 257), 2)
+                transpose_bank(
+                    src[:].bitcast(F32), cols, step, g32[:, m * 512:(m + 1) * 512], True, "wb%d_%d" % (r, m),
                 )
 
-        def mx_act(r, hh):
+        def quant(r, s):
+            if s == 0:
+                wq[r] = code_pool.tile([P, 1024], U32, name="wq%d" % r, tag="wq", align_bytes=64)
+                ws[r] = code_pool.tile([P, 1024], U8, name="ws%d" % r, tag="ws", align_bytes=64)
+            nc.vector.quantize_mx(
+                out=wq[r][:, s * 512:(s + 1) * 512].bitcast(FP8X4),
+                scales=ws[r][:, s * 512:(s + 1) * 512],
+                in_=grp[r][:, s * 2048:(s + 1) * 2048],
+            )
+
+        def mx(r, hh, s):
+            q = 2 * (r % 2) + hh
+            if s == 0:
+                accs[(r, hh)] = acc_pool.tile([P, 512], F32, name="acc%d_%d" % (r // 2, q), tag="acc")
+            for g in range(2):
+                wc = (2 * s + hh) * 256 + g * 128
+                xc = (2 * s + g) * 512
+                nc.tensor.matmul_mx(
+                    out=accs[(r, hh)][:],
+                    lhsT=wq[r][:, wc:wc + 128].bitcast(FP8X4),
+                    lhsT_scale=ws[r][:, wc:wc + 128],
+                    rhs=xq[:, xc:xc + 512].bitcast(FP8X4),
+                    rhs_scale=xs[:, xc:xc + 512],
+                    start=(s == 0 and g == 0),
+                    stop=(s == 1 and g == 1),
+                )
+
+        def act(r, hh):
             j = r // 2
             q = 2 * (r % 2) + hh
-            acc = acc_pool.tile([P, 512], F32, name="acc%d_%d" % (j, q), tag="acc")
-            for s in range(2):
-                for g in range(2):
-                    wc = (2 * hh + s) * 256 + g * 128
-                    xc = (2 * s + g) * 512
-                    nc.tensor.matmul_mx(
-                        out=acc[:],
-                        lhsT=wq[r][:, wc:wc + 128].bitcast(FP8X4),
-                        lhsT_scale=ws[r][:, wc:wc + 128],
-                        rhs=xq[:, xc:xc + 512].bitcast(FP8X4),
-                        rhs_scale=xs[:, xc:xc + 512],
-                        start=(s == 0 and g == 0),
-                        stop=(s == 1 and g == 1),
-                    )
+            acc = accs[(r, hh)]
             a = act_pool.tile([P, 512], F32, name="gate%d_%d" % (j, q), tag="gate%d" % q)
             nc.scalar.activation(
                 out=a[:], in_=acc[:], func=funcs[q],
@@ -263,34 +273,38 @@ def tile_lstmcell_kernel(
                     nc.sync.dma_start(out=out_h[:, ts, js[0] * P:(js[-1] + 1) * P], in_=outs[js][0][:, ts, :])
 
         tr_x(0, 0)
-        keep_clock(2, "idle_a")
+        keep_clock(1, "idle_a")
         tr_x(0, 1)
-        keep_clock(2, "idle_b")
-        tr_x(1, 0)
-        keep_clock(2, "idle_c")
+        keep_clock(1, "idle_b")
         quant_x(0)
+        tr_w(0, 0)
+        keep_clock(1, "idle_c")
+        quant(0, 0)
+        tr_x(1, 0)
+        keep_clock(1, "idle_d")
         tr_x(1, 1)
-        keep_clock(2, "idle_d")
+        quant_x(1)
+        mx(0, 0, 0)
+        mx(0, 1, 0)
+        tr_w(0, 1)
+        load_round(AHEAD)
 
         bsum = const.tile([P, P], F32, name="bsum")
         nc.vector.tensor_tensor(out=bsum[:], in0=braw[:, 0:P], in1=braw[:, P:2 * P], op=ALU.add)
+        permute(1)
+        quant(0, 1)
         pb = tr_pool.tile([P, 512], F32, name="pb", tag="tr")
         nc.tensor.transpose(pb[:, 0:P], bsum[:], ident[:])
         bias_sb = const.tile([P, 32], F32, name="bias_sb")
         nc.vector.tensor_copy(out=bias_sb[:], in_=pb[:, 0:32])
 
-        tr_w(0)
-        keep_clock(2, "idle_e")
-        quant_x(1)
-        quant(0)
-        load_round(AHEAD)
-        permute(1)
         for r in range(NR):
             m = r // 2
             if r + 2 < NR:
                 permute(r + 2)
             if r + 1 < NR:
-                tr_w(r + 1)
+                tr_w(r + 1, 0)
+                tr_w(r + 1, 1)
             if r % 2 == 0:
                 if m >= 1:
                     tr_out(m - 1, "f")
@@ -302,9 +316,13 @@ def tile_lstmcell_kernel(
                     ep_h(m - 1, 1)
                 mul_ig(m)
             if r + 1 < NR:
-                quant(r + 1)
-            mx_act(r, 0)
-            mx_act(r, 1)
+                quant(r + 1, 0)
+                quant(r + 1, 1)
+            for hh in range(2):
+                if r > 0:
+                    mx(r, hh, 0)
+                mx(r, hh, 1)
+                act(r, hh)
         tr_out(NT - 1, "f")
         tr_out(NT - 1, "u")
         tr_out(NT - 1, "o")

@@ -16,10 +16,10 @@ BATCH = 512
 K = 1024
 HID = 1024
 NT = HID // P
-NR = 2 * NT
 FLOPS = 2 * BATCH * (2 * K) * (4 * HID)
 
-AHEAD = 10
+NR = 2 * NT
+AHEAD = 9
 C0_AFTER = 3
 STORE_GROUPS = ((0, 1), (2, 3), (4, 5), (6,), (7,))
 TAIL_PARTS = 2
@@ -42,10 +42,10 @@ def tile_lstmcell_kernel(
 
     with ExitStack() as ctx:
         const = ctx.enter_context(tc.tile_pool(name="const", bufs=1))
-        wraw_pool = ctx.enter_context(tc.tile_pool(name="wraw", bufs=4 * AHEAD))
-        wperm_pool = ctx.enter_context(tc.tile_pool(name="wperm", bufs=8))
-        grp_pool = ctx.enter_context(tc.tile_pool(name="grp", bufs=3))
-        code_pool = ctx.enter_context(tc.tile_pool(name="code", bufs=3))
+        raw_pool = ctx.enter_context(tc.tile_pool(name="raw", bufs=2 * AHEAD + 4))
+        perm_pool = ctx.enter_context(tc.tile_pool(name="perm", bufs=6))
+        grp_pool = ctx.enter_context(tc.tile_pool(name="grp", bufs=6))
+        code_pool = ctx.enter_context(tc.tile_pool(name="code", bufs=8))
         act_pool = ctx.enter_context(tc.tile_pool(name="act", bufs=2))
         ep_pool = ctx.enter_context(tc.tile_pool(name="ep", bufs=2))
         out_pool = ctx.enter_context(tc.tile_pool(name="outp", bufs=2))
@@ -53,101 +53,122 @@ def tile_lstmcell_kernel(
         tr_pool = ctx.enter_context(tc.psum_pool(name="tr", bufs=6))
         ctx.enter_context(tc.manual_schedule())
 
-        ident = const.tile([P, P], F32, name="ident")
-        make_identity(nc, ident[:])
         zeros = const.tile([P, 512], BF16, name="zeros")
         nc.vector.memset(zeros[:], 0.0)
         warm = const.tile([P, 1], F32, name="warm")
         nc.vector.memset(warm[:], 0.0)
         braw = const.tile([P, 2 * P], BF16, name="braw")
         nc.vector.memset(braw[:], 0.0)
+        ident = const.tile([P, P], F32, name="ident")
+        make_identity(nc, ident[:])
 
         def keep_clock(n, name):
             idle = acc_pool.tile([P, 512], F32, name=name, tag="acc")
             for i in range(n):
                 nc.tensor.matmul(out=idle[:], lhsT=zeros[:, 0:P], rhs=zeros[:], start=True, stop=True)
 
-        keep_clock(6, "idle_start")
-
-        xraw = [const.tile([P, 4 * K], BF16, name="xraw%d" % s) for s in range(2)]
-
-        def load_x(s):
-            view = (x, h0)[s].rearrange("(p t) k -> p t k", t=4)
-            for th in range(2):
-                nc.sync.dma_start(
-                    out=xraw[s][:, th * 2 * K:(th + 1) * 2 * K].rearrange("p (t k) -> p t k", t=2),
-                    in_=view[:, 2 * th:2 * th + 2, :],
-                )
-
         nc.scalar.activation(out=warm[:], in_=warm[:], func=ACT.Sigmoid)
-        for q in range(4):
+
+        def load_bias(q):
             for s in range(2):
-                nc.scalar.dma_start(
+                nc.sync.dma_start(
                     out=braw[8 * q:8 * q + 8, s * P:(s + 1) * P],
                     in_=biases[q][s].rearrange("(j p) -> j p", p=P),
                 )
 
         c0_sb = const.tile([P, 4 * HID], BF16, name="c0_sb")
         c0_v = c0_sb[:].rearrange("p (t h) -> p t h", t=4)
-        wraw = {}
-        wperm = {}
+        raw = {}
 
-        def load_half(r, s):
-            j = r // 2
+        def load_x(s):
+            view = (x, h0)[s].rearrange("(p t) k -> p t k", t=4)
+            for th in range(2):
+                t = raw_pool.tile([P, 2 * K], BF16, name="x%d_%d" % (s, th), tag="raw")
+                nc.sync.dma_start(
+                    out=t[:].rearrange("p (t k) -> p t k", t=2), in_=view[:, 2 * th:2 * th + 2, :],
+                )
+                raw[("x", s, th)] = t
+
+        def load_w(j, pair, s):
+            t = raw_pool.tile([P, 2 * K], BF16, name="w%d_%d_%d" % (j, pair, s), tag="raw")
             for hh in range(2):
-                w = wraw_pool.tile([P, K], BF16, name="w%d_%d_%d" % (r, s, hh), tag="w")
-                nc.sync.dma_start(out=w[:], in_=weights[2 * (r % 2) + hh][s][j * P:(j + 1) * P, :])
-                wraw[(r, s, hh)] = w
+                nc.sync.dma_start(
+                    out=t[:, hh * K:(hh + 1) * K], in_=weights[2 * pair + hh][s][j * P:(j + 1) * P, :],
+                )
+            raw[(j, pair, s)] = t
 
         def load_round(r):
-            load_half(r, 0)
-            load_half(r, 1)
+            j, pair = divmod(r, 2)
+            for s in range(2):
+                load_w(j, pair, s)
             if r == C0_AFTER:
                 nc.sync.dma_start(out=c0_sb[:], in_=c0.rearrange("(p t) h -> p (t h)", t=4))
 
-        for s in range(2):
-            load_x(s)
-            load_half(0, s)
+        load_x(0)
+        load_w(0, 0, 0)
+        load_x(1)
+        for q in range(2):
+            load_bias(q)
+        load_w(0, 0, 1)
+        for q in range(2, 4):
+            load_bias(q)
         for r in range(1, AHEAD):
             load_round(r)
 
-        def transpose_bank(src32, cols, step, dst32, on_scalar, name):
-            bank = tr_pool.tile([P, 512], F32, name=name, tag="tr")
-            for i, c in enumerate(cols):
-                nc.tensor.transpose(bank[:, i * P:(i + 1) * P], src32[:, c:c + step * (P - 1) + 1:step], ident[:])
-            src = bank[:].rearrange("p (a u c) -> p a c u", a=2, u=2)
-            dst = dst32.rearrange("p (a c u) -> p a c u", a=2, u=2)
+        perm = {}
+        tr_banks = {}
+        grp = {}
+        wq = {}
+        ws = {}
+        xq = const.tile([P, 4 * 512], U32, name="xq", align_bytes=64)
+        xs = const.tile([P, 4 * 512], U8, name="xs", align_bytes=64)
+
+        def reorder(key):
+            t = perm_pool.tile([P, 2 * K], BF16, name="p%s_%d_%d" % key, tag="perm")
+            nc.vector.tensor_copy(
+                out=t[:].bitcast(F32).rearrange("p (g u q) -> p g u q", u=2, q=P),
+                in_=raw[key][:].bitcast(F32).rearrange("p (g q u) -> p g u q", u=2, q=P),
+            )
+            perm[key] = t
+
+        def transpose(key):
+            step = 1 if key in perm else 2
+            src = (perm if key in perm else raw)[key][:].bitcast(F32)
+            for b in range(2):
+                bank = tr_pool.tile([P, 512], F32, name="tr%s_%d_%d_%d" % (key + (b,)), tag="tr")
+                for i in range(4):
+                    c = 512 * (i // 2) + 256 * b if key[0] == "x" else 512 * b + 256 * (i // 2)
+                    c += (i % 2) * (P if step == 1 else 1)
+                    nc.tensor.transpose(
+                        bank[:, i * P:(i + 1) * P], src[:, c:c + step * (P - 1) + 1:step], ident[:],
+                    )
+                tr_banks[key + (b,)] = bank
+
+        def evacuate(key, b, on_scalar=True):
+            if key[0] == "x":
+                gkey, half = ("x", key[1], b), key[2]
+            else:
+                gkey, half = key, b
+            if gkey not in grp:
+                grp[gkey] = grp_pool.tile([P, 2048], BF16, name="g%s_%d_%d" % gkey, tag="grp", align_bytes=64)
+            src = tr_banks[key + (b,)][:].rearrange("p (a u c) -> p a c u", a=2, u=2)
+            dst = grp[gkey][:, half * 1024:(half + 1) * 1024].bitcast(F32).rearrange("p (a c u) -> p a c u", a=2, u=2)
             if on_scalar:
                 nc.scalar.copy(out=dst, in_=src)
             else:
                 nc.vector.tensor_copy(out=dst, in_=src)
 
-        xq = const.tile([P, 4 * 512], U32, name="xq", align_bytes=64)
-        xs = const.tile([P, 4 * 512], U8, name="xs", align_bytes=64)
-        xgrp = []
-        for s in range(2):
-            xg = grp_pool.tile([P, 4096], BF16, name="xgrp%d" % s, tag="grp", align_bytes=64)
-            xgrp.append(xg)
+        def quant_x(s, g):
+            c = (2 * s + g) * 512
+            nc.vector.quantize_mx(
+                out=xq[:, c:c + 512].bitcast(FP8X4), scales=xs[:, c:c + 512], in_=grp[("x", s, g)][:],
+            )
 
-        def tr_x(s, th):
-            x32 = xraw[s][:].bitcast(F32)
-            g32 = xgrp[s][:].bitcast(F32)
-            for g in range(2):
-                cols = [(2 * th + tt) * 512 + 256 * g + u for tt in range(2) for u in range(2)]
-                base = g * 1024 + th * 512
-                transpose_bank(x32, cols, 2, g32[:, base:base + 512], g == 0, "xb%d%d%d" % (s, th, g))
+        def quant(key):
+            wq[key] = code_pool.tile([P, 512], U32, name="wq%d_%d_%d" % key, tag="wq", align_bytes=64)
+            ws[key] = code_pool.tile([P, 512], U8, name="ws%d_%d_%d" % key, tag="ws", align_bytes=64)
+            nc.vector.quantize_mx(out=wq[key][:].bitcast(FP8X4), scales=ws[key][:], in_=grp[key][:])
 
-        def quant_x(s):
-            for g in range(2):
-                c = (2 * s + g) * 512
-                nc.vector.quantize_mx(
-                    out=xq[:, c:c + 512].bitcast(FP8X4), scales=xs[:, c:c + 512],
-                    in_=xgrp[s][:, g * 2048:(g + 1) * 2048],
-                )
-
-        grp = {}
-        wq = {}
-        ws = {}
         accs = {}
         gate = {}
         prod = {}
@@ -155,66 +176,29 @@ def tile_lstmcell_kernel(
         outs = {}
         tanh_c = {}
 
-        def permute(r):
-            for s in range(2):
-                for hh in range(2):
-                    w = wperm_pool.tile([P, K], BF16, name="wp%d_%d_%d" % (r, s, hh), tag="wp")
-                    nc.vector.tensor_copy(
-                        out=w[:].bitcast(F32).rearrange("p (g u q) -> p g u q", g=2, u=2),
-                        in_=wraw[(r, s, hh)][:].bitcast(F32).rearrange("p (g q u) -> p g u q", g=2, u=2),
-                    )
-                    wperm[(r, s, hh)] = w
-            if r + AHEAD < NR:
-                load_round(r + AHEAD)
-
-        def tr_w(r, s):
+        def mx(j, q, s):
+            key = (j, q // 2, s)
             if s == 0:
-                grp[r] = grp_pool.tile([P, 4096], BF16, name="grp%d" % r, tag="grp", align_bytes=64)
-            g32 = grp[r][:].bitcast(F32)
-            for hh in range(2):
-                key = (r, s, hh)
-                m = 2 * s + hh
-                src, cols, step = (wperm[key], (0, 128, 256, 384), 1) if key in wperm else (wraw[key], (0, 1, 256, 257), 2)
-                transpose_bank(
-                    src[:].bitcast(F32), cols, step, g32[:, m * 512:(m + 1) * 512], True, "wb%d_%d" % (r, m),
-                )
-
-        def quant(r, s):
-            if s == 0:
-                wq[r] = code_pool.tile([P, 1024], U32, name="wq%d" % r, tag="wq", align_bytes=64)
-                ws[r] = code_pool.tile([P, 1024], U8, name="ws%d" % r, tag="ws", align_bytes=64)
-            nc.vector.quantize_mx(
-                out=wq[r][:, s * 512:(s + 1) * 512].bitcast(FP8X4),
-                scales=ws[r][:, s * 512:(s + 1) * 512],
-                in_=grp[r][:, s * 2048:(s + 1) * 2048],
-            )
-
-        def mx(r, hh, s):
-            q = 2 * (r % 2) + hh
-            if s == 0:
-                accs[(r, hh)] = acc_pool.tile([P, 512], F32, name="acc%d_%d" % (r // 2, q), tag="acc")
+                accs[(j, q)] = acc_pool.tile([P, 512], F32, name="acc%d_%d" % (j, q), tag="acc")
             for g in range(2):
-                wc = (2 * s + hh) * 256 + g * 128
+                wc = (q % 2) * 256 + g * 128
                 xc = (2 * s + g) * 512
                 nc.tensor.matmul_mx(
-                    out=accs[(r, hh)][:],
-                    lhsT=wq[r][:, wc:wc + 128].bitcast(FP8X4),
-                    lhsT_scale=ws[r][:, wc:wc + 128],
-                    rhs=xq[:, xc:xc + 512].bitcast(FP8X4),
-                    rhs_scale=xs[:, xc:xc + 512],
-                    start=(s == 0 and g == 0),
-                    stop=(s == 1 and g == 1),
+                    out=accs[(j, q)][:],
+                    lhsT=wq[key][:, wc:wc + 128].bitcast(FP8X4), lhsT_scale=ws[key][:, wc:wc + 128],
+                    rhs=xq[:, xc:xc + 512].bitcast(FP8X4), rhs_scale=xs[:, xc:xc + 512],
+                    start=(s == 0 and g == 0), stop=(s == 1 and g == 1),
                 )
 
-        def act(r, hh):
-            j = r // 2
-            q = 2 * (r % 2) + hh
-            acc = accs[(r, hh)]
+        def act(j, q, parts=1):
             a = act_pool.tile([P, 512], F32, name="gate%d_%d" % (j, q), tag="gate%d" % q)
-            nc.scalar.activation(
-                out=a[:], in_=acc[:], func=funcs[q],
-                bias=bias_sb[:, 8 * q + j:8 * q + j + 1], scale=1.0,
-            )
+            n = 512 // parts
+            for part in range(parts):
+                cs = slice(part * n, (part + 1) * n)
+                nc.scalar.activation(
+                    out=a[:, cs], in_=accs[(j, q)][:, cs], func=funcs[q],
+                    bias=bias_sb[:, 8 * q + j:8 * q + j + 1], scale=1.0,
+                )
             gate[(j, q)] = a
 
         def mul_ig(j):
@@ -222,20 +206,17 @@ def tile_lstmcell_kernel(
             nc.vector.tensor_tensor(out=t[:], in0=gate[(j, 0)][:], in1=gate[(j, 1)][:], op=ALU.mult)
             prod[j] = t
 
-        def tr_out(j, key):
-            src = {"f": gate[(j, 2)], "u": prod[j], "o": gate[(j, 3)]}[key]
-            bank = tr_pool.tile([P, 512], F32, name="ob%s%d" % (key, j), tag="tr")
+        def tr_out(j, what):
+            src = {"f": gate.get((j, 2)), "u": prod.get(j), "o": gate.get((j, 3))}[what]
+            bank = tr_pool.tile([P, 512], F32, name="ob%s%d" % (what, j), tag="tr")
             for t in range(4):
                 nc.tensor.transpose(bank[:, t * P:(t + 1) * P], src[:, t * P:(t + 1) * P], ident[:])
-            banks[(j, key)] = bank[:].rearrange("p (t h) -> p t h", t=4)
+            banks[(j, what)] = bank[:].rearrange("p (t h) -> p t h", t=4)
 
         def group_of(j):
-            for grp_js in STORE_GROUPS:
-                if j in grp_js:
-                    return grp_js
-            return None
+            return [js for js in STORE_GROUPS if j in js][0]
 
-        def ep_c(j, parts):
+        def cell(j, parts):
             js = group_of(j)
             width = P * len(js)
             if j == js[0]:
@@ -245,7 +226,6 @@ def tile_lstmcell_kernel(
                 )
             off = (j - js[0]) * P
             t1 = ep_pool.tile([P, 4, P], F32, name="t1_%d" % j, tag="t1")
-            th = ep_pool.tile([P, 4, P], F32, name="th%d" % j, tag="th")
             n = 4 // parts
             for part in range(parts):
                 ts = slice(part * n, (part + 1) * n)
@@ -254,12 +234,20 @@ def tile_lstmcell_kernel(
                     out=t1[:, ts, :], in0=banks[(j, "f")][:, ts, :], in1=c0_v[:, ts, j * P:(j + 1) * P], op=ALU.mult,
                 )
                 nc.vector.tensor_tensor(out=oc_v, in0=banks[(j, "u")][:, ts, :], in1=t1[:, ts, :], op=ALU.add)
-                nc.scalar.activation(out=th[:, ts, :], in_=oc_v, func=ACT.Tanh)
-            tanh_c[j] = th
             if j == js[-1]:
                 nc.sync.dma_start(out=out_c[:, :, js[0] * P:(js[-1] + 1) * P], in_=outs[js][1][:])
 
-        def ep_h(j, parts):
+        def tanh_cell(j, parts):
+            js = group_of(j)
+            off = (j - js[0]) * P
+            th = ep_pool.tile([P, 4, P], F32, name="th%d" % j, tag="th")
+            n = 4 // parts
+            for part in range(parts):
+                ts = slice(part * n, (part + 1) * n)
+                nc.scalar.activation(out=th[:, ts, :], in_=outs[js][1][:, ts, off:off + P], func=ACT.Tanh)
+            tanh_c[j] = th
+
+        def hidden(j, parts):
             js = group_of(j)
             off = (j - js[0]) * P
             n = 4 // parts
@@ -272,59 +260,81 @@ def tile_lstmcell_kernel(
                 if j == js[-1]:
                     nc.sync.dma_start(out=out_h[:, ts, js[0] * P:(js[-1] + 1) * P], in_=outs[js][0][:, ts, :])
 
-        tr_x(0, 0)
+        def do_x(s, th, share):
+            key = ("x", s, th)
+            transpose(key)
+            evacuate(key, 0)
+            evacuate(key, 1, on_scalar=not share)
+
+        def do_w(key):
+            transpose(key)
+            for b in range(2):
+                evacuate(key, b)
+
+        keep_clock(6, "idle_start")
+        do_x(0, 0, True)
         keep_clock(1, "idle_a")
-        tr_x(0, 1)
+        do_x(0, 1, True)
         keep_clock(1, "idle_b")
-        quant_x(0)
-        tr_w(0, 0)
+        quant_x(0, 0)
+        quant_x(0, 1)
+        do_w((0, 0, 0))
+        quant((0, 0, 0))
+        do_x(1, 0, False)
         keep_clock(1, "idle_c")
-        quant(0, 0)
-        tr_x(1, 0)
-        keep_clock(1, "idle_d")
-        tr_x(1, 1)
-        quant_x(1)
-        mx(0, 0, 0)
-        mx(0, 1, 0)
-        tr_w(0, 1)
-        load_round(AHEAD)
+        do_x(1, 1, False)
+        reorder((0, 0, 1))
+        reorder((0, 1, 0))
+        for q in range(2):
+            mx(0, q, 0)
+        do_w((0, 0, 1))
+        quant_x(1, 0)
+        quant_x(1, 1)
+        reorder((0, 1, 1))
 
         bsum = const.tile([P, P], F32, name="bsum")
         nc.vector.tensor_tensor(out=bsum[:], in0=braw[:, 0:P], in1=braw[:, P:2 * P], op=ALU.add)
-        permute(1)
-        quant(0, 1)
+        quant((0, 0, 1))
+
+        for s in range(2):
+            do_w((0, 1, s))
         pb = tr_pool.tile([P, 512], F32, name="pb", tag="tr")
         nc.tensor.transpose(pb[:, 0:P], bsum[:], ident[:])
         bias_sb = const.tile([P, 32], F32, name="bias_sb")
         nc.vector.tensor_copy(out=bias_sb[:], in_=pb[:, 0:32])
 
         for r in range(NR):
-            m = r // 2
+            j, pair = divmod(r, 2)
             if r + 2 < NR:
-                permute(r + 2)
-            if r + 1 < NR:
-                tr_w(r + 1, 0)
-                tr_w(r + 1, 1)
-            if r % 2 == 0:
-                if m >= 1:
-                    tr_out(m - 1, "f")
-                    tr_out(m - 1, "u")
-                    ep_c(m - 1, 1)
+                for s in range(2):
+                    reorder(divmod(r + 2, 2) + (s,))
+            if 0 < r < NR - 1:
+                for s in range(2):
+                    do_w(divmod(r + 1, 2) + (s,))
+            if pair == 0:
+                if j > 0:
+                    tr_out(j - 1, "f")
+                    tr_out(j - 1, "u")
+                    cell(j - 1, 1)
+                    tanh_cell(j - 1, 1)
             else:
-                if m >= 1:
-                    tr_out(m - 1, "o")
-                    ep_h(m - 1, 1)
-                mul_ig(m)
+                if j > 0:
+                    tr_out(j - 1, "o")
+                    hidden(j - 1, 1)
+                mul_ig(j)
             if r + 1 < NR:
-                quant(r + 1, 0)
-                quant(r + 1, 1)
-            for hh in range(2):
+                for s in range(2):
+                    quant(divmod(r + 1, 2) + (s,))
+            for q in (2 * pair, 2 * pair + 1):
                 if r > 0:
-                    mx(r, hh, 0)
-                mx(r, hh, 1)
-                act(r, hh)
+                    mx(j, q, 0)
+                mx(j, q, 1)
+                act(j, q)
+            if r + AHEAD < NR:
+                load_round(r + AHEAD)
         tr_out(NT - 1, "f")
         tr_out(NT - 1, "u")
         tr_out(NT - 1, "o")
-        ep_c(NT - 1, TAIL_PARTS)
-        ep_h(NT - 1, TAIL_PARTS)
+        cell(NT - 1, TAIL_PARTS)
+        tanh_cell(NT - 1, TAIL_PARTS)
+        hidden(NT - 1, TAIL_PARTS)

@@ -126,8 +126,8 @@ def tile_lstmcell_kernel(
         def reorder(key):
             t = perm_pool.tile([P, 2 * K], BF16, name="p%s_%d_%d" % key, tag="perm")
             nc.vector.tensor_copy(
-                out=t[:].bitcast(F32).rearrange("p (g u q) -> p g u q", u=2, q=P),
-                in_=raw[key][:].bitcast(F32).rearrange("p (g q u) -> p g u q", u=2, q=P),
+                out=t[:].bitcast(F32).rearrange("p (g u b i) -> p g b u i", u=2, b=32, i=4),
+                in_=raw[key][:].bitcast(F32).rearrange("p (g b i u) -> p g b u i", u=2, b=32, i=4),
             )
             perm[key] = t
 

@@ -20,7 +20,7 @@ FLOPS = 2 * BATCH * (2 * K) * (4 * HID)
 
 NR = 2 * NT
 AHEAD = 9
-C0_AFTER = 3
+C0_AFTER = (3, 7)
 STORE_GROUPS = ((0, 1), (2, 3), (4, 5), (6,), (7,))
 TAIL_PARTS = 2
 
@@ -50,7 +50,8 @@ def tile_lstmcell_kernel(
         ep_pool = ctx.enter_context(tc.tile_pool(name="ep", bufs=2))
         out_pool = ctx.enter_context(tc.tile_pool(name="outp", bufs=2))
         acc_pool = ctx.enter_context(tc.psum_pool(name="acc", bufs=2))
-        tr_pool = ctx.enter_context(tc.psum_pool(name="tr", bufs=6))
+        back_pool = ctx.enter_context(tc.psum_pool(name="back", bufs=2))
+        tr_pool = ctx.enter_context(tc.psum_pool(name="tr", bufs=4))
         ctx.enter_context(tc.manual_schedule())
 
         zeros = const.tile([P, 512], BF16, name="zeros")
@@ -71,13 +72,12 @@ def tile_lstmcell_kernel(
 
         def load_bias(q):
             for s in range(2):
-                nc.sync.dma_start(
+                nc.gpsimd.dma_start(
                     out=braw[8 * q:8 * q + 8, s * P:(s + 1) * P],
                     in_=biases[q][s].rearrange("(j p) -> j p", p=P),
                 )
 
-        c0_sb = const.tile([P, 4 * HID], BF16, name="c0_sb")
-        c0_v = c0_sb[:].rearrange("p (t h) -> p t h", t=4)
+        c0_half = [const.tile([P, 4, HID // 2], BF16, name="c0_%d" % half) for half in range(2)]
         raw = {}
 
         def load_x(s):
@@ -101,18 +101,20 @@ def tile_lstmcell_kernel(
             j, pair = divmod(r, 2)
             for s in range(2):
                 load_w(j, pair, s)
-            if r == C0_AFTER:
-                nc.sync.dma_start(out=c0_sb[:], in_=c0.rearrange("(p t) h -> p (t h)", t=4))
+            if r in C0_AFTER:
+                half = C0_AFTER.index(r)
+                nc.sync.dma_start(
+                    out=c0_half[half][:],
+                    in_=c0.rearrange("(p t) h -> p t h", t=4)[:, :, half * (HID // 2):(half + 1) * (HID // 2)],
+                )
 
-        load_x(0)
-        load_w(0, 0, 0)
-        load_x(1)
-        for q in range(2):
+        for q in range(4):
             load_bias(q)
-        load_w(0, 0, 1)
-        for q in range(2, 4):
-            load_bias(q)
-        for r in range(1, AHEAD):
+        for s in range(2):
+            load_x(s)
+            for pair in range(2):
+                load_w(0, pair, s)
+        for r in range(2, AHEAD):
             load_round(r)
 
         perm = {}
@@ -123,12 +125,15 @@ def tile_lstmcell_kernel(
         xq = const.tile([P, 4 * 512], U32, name="xq", align_bytes=64)
         xs = const.tile([P, 4 * 512], U8, name="xs", align_bytes=64)
 
-        def reorder(key):
+        def reorder(key, parts=1):
             t = perm_pool.tile([P, 2 * K], BF16, name="p%s_%d_%d" % key, tag="perm")
-            nc.vector.tensor_copy(
-                out=t[:].bitcast(F32).rearrange("p (g u b i) -> p g b u i", u=2, b=32, i=4),
-                in_=raw[key][:].bitcast(F32).rearrange("p (g b i u) -> p g b u i", u=2, b=32, i=4),
-            )
+            n = 2 * K // parts
+            for part in range(parts):
+                cs = slice(part * n, (part + 1) * n)
+                nc.vector.tensor_copy(
+                    out=t[:, cs].bitcast(F32).rearrange("p (g u b i) -> p g b u i", u=2, b=32, i=4),
+                    in_=raw[key][:, cs].bitcast(F32).rearrange("p (g b i u) -> p g b u i", u=2, b=32, i=4),
+                )
             perm[key] = t
 
         def transpose(key):
@@ -179,7 +184,8 @@ def tile_lstmcell_kernel(
         def mx(j, q, s):
             key = (j, q // 2, s)
             if s == 0:
-                accs[(j, q)] = acc_pool.tile([P, 512], F32, name="acc%d_%d" % (j, q), tag="acc")
+                pool, tag = (back_pool, "back") if j == 0 and q >= 2 else (acc_pool, "acc")
+                accs[(j, q)] = pool.tile([P, 512], F32, name="acc%d_%d" % (j, q), tag=tag)
             for g in range(2):
                 wc = (q % 2) * 256 + g * 128
                 xc = (2 * s + g) * 512
@@ -208,7 +214,7 @@ def tile_lstmcell_kernel(
 
         def tr_out(j, what):
             src = {"f": gate.get((j, 2)), "u": prod.get(j), "o": gate.get((j, 3))}[what]
-            bank = tr_pool.tile([P, 512], F32, name="ob%s%d" % (what, j), tag="tr")
+            bank = back_pool.tile([P, 512], F32, name="ob%s%d" % (what, j), tag="back")
             for t in range(4):
                 nc.tensor.transpose(bank[:, t * P:(t + 1) * P], src[:, t * P:(t + 1) * P], ident[:])
             banks[(j, what)] = bank[:].rearrange("p (t h) -> p t h", t=4)
@@ -231,7 +237,7 @@ def tile_lstmcell_kernel(
                 ts = slice(part * n, (part + 1) * n)
                 oc_v = outs[js][1][:, ts, off:off + P]
                 nc.vector.tensor_tensor(
-                    out=t1[:, ts, :], in0=banks[(j, "f")][:, ts, :], in1=c0_v[:, ts, j * P:(j + 1) * P], op=ALU.mult,
+                    out=t1[:, ts, :], in0=banks[(j, "f")][:, ts, :], in1=c0_half[j // 4][:, ts, (j % 4) * P:(j % 4 + 1) * P], op=ALU.mult,
                 )
                 nc.vector.tensor_tensor(out=oc_v, in0=banks[(j, "u")][:, ts, :], in1=t1[:, ts, :], op=ALU.add)
             if j == js[-1]:
@@ -276,28 +282,29 @@ def tile_lstmcell_kernel(
         keep_clock(1, "idle_a")
         do_x(0, 1, True)
         keep_clock(1, "idle_b")
+        do_w((0, 0, 0))
         quant_x(0, 0)
         quant_x(0, 1)
-        do_w((0, 0, 0))
+        do_w((0, 1, 0))
         quant((0, 0, 0))
         do_x(1, 0, False)
-        keep_clock(1, "idle_c")
-        do_x(1, 1, False)
-        reorder((0, 0, 1))
-        reorder((0, 1, 0))
+        quant((0, 1, 0))
         for q in range(2):
             mx(0, q, 0)
+        do_x(1, 1, False)
+        reorder((0, 0, 1), 2)
         do_w((0, 0, 1))
+        reorder((0, 1, 1), 2)
+        for q in range(2, 4):
+            mx(0, q, 0)
         quant_x(1, 0)
         quant_x(1, 1)
-        reorder((0, 1, 1))
 
         bsum = const.tile([P, P], F32, name="bsum")
         nc.vector.tensor_tensor(out=bsum[:], in0=braw[:, 0:P], in1=braw[:, P:2 * P], op=ALU.add)
+        do_w((0, 1, 1))
+        reorder((1, 0, 0), 2)
         quant((0, 0, 1))
-
-        for s in range(2):
-            do_w((0, 1, s))
         pb = tr_pool.tile([P, 512], F32, name="pb", tag="tr")
         nc.tensor.transpose(pb[:, 0:P], bsum[:], ident[:])
         bias_sb = const.tile([P, 32], F32, name="bias_sb")
@@ -306,7 +313,7 @@ def tile_lstmcell_kernel(
         for r in range(NR):
             j, pair = divmod(r, 2)
             if r + 2 < NR:
-                for s in range(2):
+                for s in range(1 if r == 0 else 0, 2):
                     reorder(divmod(r + 2, 2) + (s,))
             if 0 < r < NR - 1:
                 for s in range(2):
@@ -323,10 +330,10 @@ def tile_lstmcell_kernel(
                     hidden(j - 1, 1)
                 mul_ig(j)
             if r + 1 < NR:
-                for s in range(2):
+                for s in range(1 if r == 0 else 0, 2):
                     quant(divmod(r + 1, 2) + (s,))
             for q in (2 * pair, 2 * pair + 1):
-                if r > 0:
+                if r > 1:
                     mx(j, q, 0)
                 mx(j, q, 1)
                 act(j, q)

@@ -21,8 +21,7 @@ FLOPS = 2 * BATCH * (2 * K) * (4 * HID)
 NR = 2 * NT
 AHEAD = 9
 C0_AFTER = (3, 7)
-STORE_GROUPS = ((0, 1), (2, 3), (4, 5), (6,), (7,))
-TAIL_PARTS = 2
+STORE_GROUPS = ((0, 1), (2, 3), (4, 5), (6,))
 
 
 def tile_lstmcell_kernel(
@@ -49,6 +48,7 @@ def tile_lstmcell_kernel(
         act_pool = ctx.enter_context(tc.tile_pool(name="act", bufs=2))
         ep_pool = ctx.enter_context(tc.tile_pool(name="ep", bufs=2))
         out_pool = ctx.enter_context(tc.tile_pool(name="outp", bufs=2))
+        last_pool = ctx.enter_context(tc.tile_pool(name="last", bufs=2))
         acc_pool = ctx.enter_context(tc.psum_pool(name="acc", bufs=2))
         back_pool = ctx.enter_context(tc.psum_pool(name="back", bufs=2))
         tr_pool = ctx.enter_context(tc.psum_pool(name="tr", bufs=4))
@@ -196,15 +196,11 @@ def tile_lstmcell_kernel(
                     start=(s == 0 and g == 0), stop=(s == 1 and g == 1),
                 )
 
-        def act(j, q, parts=1):
+        def act(j, q):
             a = act_pool.tile([P, 512], F32, name="gate%d_%d" % (j, q), tag="gate%d" % q)
-            n = 512 // parts
-            for part in range(parts):
-                cs = slice(part * n, (part + 1) * n)
-                nc.scalar.activation(
-                    out=a[:, cs], in_=accs[(j, q)][:, cs], func=funcs[q],
-                    bias=bias_sb[:, 8 * q + j:8 * q + j + 1], scale=1.0,
-                )
+            nc.scalar.activation(
+                out=a[:], in_=accs[(j, q)][:], func=funcs[q], bias=bias_sb[:, 8 * q + j:8 * q + j + 1], scale=1.0,
+            )
             gate[(j, q)] = a
 
         def mul_ig(j):
@@ -212,9 +208,9 @@ def tile_lstmcell_kernel(
             nc.vector.tensor_tensor(out=t[:], in0=gate[(j, 0)][:], in1=gate[(j, 1)][:], op=ALU.mult)
             prod[j] = t
 
-        def tr_out(j, what):
+        def tr_out(j, what, pool=back_pool, tag="back"):
             src = {"f": gate.get((j, 2)), "u": prod.get(j), "o": gate.get((j, 3))}[what]
-            bank = back_pool.tile([P, 512], F32, name="ob%s%d" % (what, j), tag="back")
+            bank = pool.tile([P, 512], F32, name="ob%s%d" % (what, j), tag=tag)
             for t in range(4):
                 nc.tensor.transpose(bank[:, t * P:(t + 1) * P], src[:, t * P:(t + 1) * P], ident[:])
             banks[(j, what)] = bank[:].rearrange("p (t h) -> p t h", t=4)
@@ -222,7 +218,7 @@ def tile_lstmcell_kernel(
         def group_of(j):
             return [js for js in STORE_GROUPS if j in js][0]
 
-        def cell(j, parts):
+        def cell(j):
             js = group_of(j)
             width = P * len(js)
             if j == js[0]:
@@ -232,39 +228,27 @@ def tile_lstmcell_kernel(
                 )
             off = (j - js[0]) * P
             t1 = ep_pool.tile([P, 4, P], F32, name="t1_%d" % j, tag="t1")
-            n = 4 // parts
-            for part in range(parts):
-                ts = slice(part * n, (part + 1) * n)
-                oc_v = outs[js][1][:, ts, off:off + P]
-                nc.vector.tensor_tensor(
-                    out=t1[:, ts, :], in0=banks[(j, "f")][:, ts, :], in1=c0_half[j // 4][:, ts, (j % 4) * P:(j % 4 + 1) * P], op=ALU.mult,
-                )
-                nc.vector.tensor_tensor(out=oc_v, in0=banks[(j, "u")][:, ts, :], in1=t1[:, ts, :], op=ALU.add)
+            nc.vector.tensor_tensor(
+                out=t1[:], in0=banks[(j, "f")], in1=c0_half[j // 4][:, :, (j % 4) * P:(j % 4 + 1) * P], op=ALU.mult,
+            )
+            nc.vector.tensor_tensor(out=outs[js][1][:, :, off:off + P], in0=banks[(j, "u")], in1=t1[:], op=ALU.add)
             if j == js[-1]:
                 nc.sync.dma_start(out=out_c[:, :, js[0] * P:(js[-1] + 1) * P], in_=outs[js][1][:])
 
-        def tanh_cell(j, parts):
+        def tanh_cell(j):
             js = group_of(j)
             off = (j - js[0]) * P
-            th = ep_pool.tile([P, 4, P], F32, name="th%d" % j, tag="th")
-            n = 4 // parts
-            for part in range(parts):
-                ts = slice(part * n, (part + 1) * n)
-                nc.scalar.activation(out=th[:, ts, :], in_=outs[js][1][:, ts, off:off + P], func=ACT.Tanh)
-            tanh_c[j] = th
+            tanh_c[j] = ep_pool.tile([P, 4, P], F32, name="th%d" % j, tag="th")
+            nc.scalar.activation(out=tanh_c[j][:], in_=outs[js][1][:, :, off:off + P], func=ACT.Tanh)
 
-        def hidden(j, parts):
+        def hidden(j):
             js = group_of(j)
             off = (j - js[0]) * P
-            n = 4 // parts
-            for part in range(parts):
-                ts = slice(part * n, (part + 1) * n)
-                nc.vector.tensor_tensor(
-                    out=outs[js][0][:, ts, off:off + P], in0=banks[(j, "o")][:, ts, :], in1=tanh_c[j][:, ts, :],
-                    op=ALU.mult,
-                )
-                if j == js[-1]:
-                    nc.sync.dma_start(out=out_h[:, ts, js[0] * P:(js[-1] + 1) * P], in_=outs[js][0][:, ts, :])
+            nc.vector.tensor_tensor(
+                out=outs[js][0][:, :, off:off + P], in0=banks[(j, "o")], in1=tanh_c[j][:], op=ALU.mult,
+            )
+            if j == js[-1]:
+                nc.sync.dma_start(out=out_h[:, :, js[0] * P:(js[-1] + 1) * P], in_=outs[js][0][:])
 
         def do_x(s, th, share):
             key = ("x", s, th)
@@ -277,7 +261,7 @@ def tile_lstmcell_kernel(
             for b in range(2):
                 evacuate(key, b)
 
-        keep_clock(6, "idle_start")
+        keep_clock(10, "idle_start")
         do_x(0, 0, True)
         keep_clock(1, "idle_a")
         do_x(0, 1, True)
@@ -310,28 +294,26 @@ def tile_lstmcell_kernel(
         bias_sb = const.tile([P, 32], F32, name="bias_sb")
         nc.vector.tensor_copy(out=bias_sb[:], in_=pb[:, 0:32])
 
-        for r in range(NR):
+        for r in range(NR - 2):
             j, pair = divmod(r, 2)
-            if r + 2 < NR:
-                for s in range(1 if r == 0 else 0, 2):
-                    reorder(divmod(r + 2, 2) + (s,))
-            if 0 < r < NR - 1:
+            for s in range(1 if r == 0 else 0, 2):
+                reorder(divmod(r + 2, 2) + (s,))
+            if r > 0:
                 for s in range(2):
                     do_w(divmod(r + 1, 2) + (s,))
             if pair == 0:
                 if j > 0:
                     tr_out(j - 1, "f")
                     tr_out(j - 1, "u")
-                    cell(j - 1, 1)
-                    tanh_cell(j - 1, 1)
+                    cell(j - 1)
+                    tanh_cell(j - 1)
             else:
                 if j > 0:
                     tr_out(j - 1, "o")
-                    hidden(j - 1, 1)
+                    hidden(j - 1)
                 mul_ig(j)
-            if r + 1 < NR:
-                for s in range(1 if r == 0 else 0, 2):
-                    quant(divmod(r + 1, 2) + (s,))
+            for s in range(1 if r == 0 else 0, 2):
+                quant(divmod(r + 1, 2) + (s,))
             for q in (2 * pair, 2 * pair + 1):
                 if r > 1:
                     mx(j, q, 0)
@@ -339,9 +321,91 @@ def tile_lstmcell_kernel(
                 act(j, q)
             if r + AHEAD < NR:
                 load_round(r + AHEAD)
-        tr_out(NT - 1, "f")
-        tr_out(NT - 1, "u")
-        tr_out(NT - 1, "o")
-        cell(NT - 1, TAIL_PARTS)
-        tanh_cell(NT - 1, TAIL_PARTS)
-        hidden(NT - 1, TAIL_PARTS)
+
+        j = NT - 1
+        cols = slice(j * P, (j + 1) * P)
+        part = {}
+
+        def half_gate(half, q, pool, tag):
+            acc = pool.tile([P, 512], F32, name="accl%d_%d" % (half, q), tag=tag)
+            for s in range(2):
+                key = (j, q // 2, s)
+                for g in range(2):
+                    wc = (q % 2) * 256 + g * 128
+                    xc = (2 * s + g) * 512 + half * 256
+                    nc.tensor.matmul_mx(
+                        out=acc[:, 0:256],
+                        lhsT=wq[key][:, wc:wc + 128].bitcast(FP8X4), lhsT_scale=ws[key][:, wc:wc + 128],
+                        rhs=xq[:, xc:xc + 256].bitcast(FP8X4), rhs_scale=xs[:, xc:xc + 256],
+                        start=(s == 0 and g == 0), stop=(s == 1 and g == 1),
+                    )
+            a = last_pool.tile([P, 256], F32, name="gatel%d_%d" % (half, q), tag="g%d" % q)
+            nc.scalar.activation(
+                out=a[:], in_=acc[:, 0:256], func=funcs[q], bias=bias_sb[:, 8 * q + j:8 * q + j + 1], scale=1.0,
+            )
+            part[(half, q)] = a
+
+        def half_ig(half):
+            part[(half, "u")] = last_pool.tile([P, 256], F32, name="igl%d" % half, tag="u")
+            nc.vector.tensor_tensor(
+                out=part[(half, "u")][:], in0=part[(half, 0)][:], in1=part[(half, 1)][:], op=ALU.mult,
+            )
+
+        def half_out(half, what, pool, tag):
+            bank = pool.tile([P, 512], F32, name="obl%d_%s" % (half, what), tag=tag)
+            for t in range(2):
+                nc.tensor.transpose(bank[:, t * P:(t + 1) * P], part[(half, what)][:, t * P:(t + 1) * P], ident[:])
+            banks[(half, what)] = bank[:, 0:256].rearrange("p (t h) -> p t h", t=2)
+
+        def half_cell(half):
+            ts = slice(2 * half, 2 * half + 2)
+            t1 = last_pool.tile([P, 2, P], F32, name="t1l%d" % half, tag="t1")
+            c = last_pool.tile([P, 2, P], F32, name="cl%d" % half, tag="c")
+            nc.vector.tensor_tensor(
+                out=t1[:], in0=banks[(half, 2)], in1=c0_half[1][:, ts, HID // 2 - P:HID // 2], op=ALU.mult,
+            )
+            nc.vector.tensor_tensor(out=c[:], in0=banks[(half, "u")], in1=t1[:], op=ALU.add)
+            nc.sync.dma_start(out=out_c[:, ts, cols], in_=c[:])
+            part[(half, "c")] = c
+
+        def half_tanh(half):
+            part[(half, "th")] = last_pool.tile([P, 2, P], F32, name="thl%d" % half, tag="th")
+            nc.scalar.activation(out=part[(half, "th")][:], in_=part[(half, "c")][:], func=ACT.Tanh)
+
+        def half_hidden(half):
+            h = last_pool.tile([P, 2, P], F32, name="hl%d" % half, tag="h")
+            nc.vector.tensor_tensor(out=h[:], in0=banks[(half, 3)], in1=part[(half, "th")][:], op=ALU.mult)
+            nc.sync.dma_start(out=out_h[:, 2 * half:2 * half + 2, cols], in_=h[:])
+
+        for s in range(2):
+            do_w((j, 1, s))
+        tr_out(j - 1, "f")
+        tr_out(j - 1, "u")
+        cell(j - 1)
+        tr_out(j - 1, "o", tr_pool, "tr")
+        for s in range(2):
+            quant((j, 1, s))
+        half_gate(0, 0, acc_pool, "acc")
+        half_gate(0, 1, acc_pool, "acc")
+        tanh_cell(j - 1)
+        half_ig(0)
+        hidden(j - 1)
+        half_gate(1, 0, back_pool, "back")
+        half_gate(1, 1, back_pool, "back")
+        half_ig(1)
+        half_gate(0, 2, tr_pool, "tr")
+        half_gate(0, 3, tr_pool, "tr")
+        half_gate(1, 2, tr_pool, "tr")
+        half_out(0, 2, acc_pool, "acc")
+        half_out(0, "u", acc_pool, "acc")
+        half_cell(0)
+        half_tanh(0)
+        half_out(0, 3, tr_pool, "tr")
+        half_out(1, "u", tr_pool, "tr")
+        half_out(1, 2, tr_pool, "tr")
+        half_cell(1)
+        half_gate(1, 3, tr_pool, "tr")
+        half_hidden(0)
+        half_tanh(1)
+        half_out(1, 3, back_pool, "back")
+        half_hidden(1)

@@ -15,13 +15,14 @@ P = 128
 BATCH = 512
 K = 1024
 HID = 1024
-NT = HID // P
 FLOPS = 2 * BATCH * (2 * K) * (4 * HID)
 
-NR = 2 * NT
-AHEAD = 9
+NT = HID // P
+NM = NT // 2
+NR = 4 * NM
+AHEAD = 8
 C0_AFTER = (3, 7)
-STORE_GROUPS = ((0, 1), (2, 3), (4, 5), (6,))
+BIAS_O_AFTER = 4
 
 
 def tile_lstmcell_kernel(
@@ -39,16 +40,25 @@ def tile_lstmcell_kernel(
     out_h = out_0.rearrange("(p t) h -> p t h", t=4)
     out_c = out_1.rearrange("(p t) h -> p t h", t=4)
 
+    def parts_of(r):
+        m, kind = divmod(r, 4)
+        if kind == 0:
+            return ((0, 2 * m), (1, 2 * m))
+        if kind == 1:
+            return ((2, 2 * m), (2, 2 * m + 1))
+        if kind == 2:
+            return ((0, 2 * m + 1), (1, 2 * m + 1))
+        return ((3, 2 * m), (3, 2 * m + 1))
+
     with ExitStack() as ctx:
         const = ctx.enter_context(tc.tile_pool(name="const", bufs=1))
         raw_pool = ctx.enter_context(tc.tile_pool(name="raw", bufs=2 * AHEAD + 4))
-        perm_pool = ctx.enter_context(tc.tile_pool(name="perm", bufs=6))
+        perm_pool = ctx.enter_context(tc.tile_pool(name="perm", bufs=5))
         grp_pool = ctx.enter_context(tc.tile_pool(name="grp", bufs=6))
-        code_pool = ctx.enter_context(tc.tile_pool(name="code", bufs=8))
-        act_pool = ctx.enter_context(tc.tile_pool(name="act", bufs=2))
+        code_pool = ctx.enter_context(tc.tile_pool(name="code", bufs=6))
+        act_pool = ctx.enter_context(tc.tile_pool(name="act", bufs=3))
         ep_pool = ctx.enter_context(tc.tile_pool(name="ep", bufs=2))
         out_pool = ctx.enter_context(tc.tile_pool(name="outp", bufs=2))
-        last_pool = ctx.enter_context(tc.tile_pool(name="last", bufs=2))
         acc_pool = ctx.enter_context(tc.psum_pool(name="acc", bufs=2))
         back_pool = ctx.enter_context(tc.psum_pool(name="back", bufs=2))
         tr_pool = ctx.enter_context(tc.psum_pool(name="tr", bufs=4))
@@ -62,6 +72,10 @@ def tile_lstmcell_kernel(
         nc.vector.memset(braw[:], 0.0)
         ident = const.tile([P, P], F32, name="ident")
         make_identity(nc, ident[:])
+        ones = const.tile([P, P], BF16, name="ones")
+        nc.gpsimd.memset(ones[:], 1.0)
+        orow = const.tile([P, HID], BF16, name="orow")
+        nc.gpsimd.memset(orow[:], 0.0)
 
         def keep_clock(n, name):
             idle = acc_pool.tile([P, 512], F32, name=name, tag="acc")
@@ -69,6 +83,8 @@ def tile_lstmcell_kernel(
                 nc.tensor.matmul(out=idle[:], lhsT=zeros[:, 0:P], rhs=zeros[:], start=True, stop=True)
 
         nc.scalar.activation(out=warm[:], in_=warm[:], func=ACT.Sigmoid)
+        c0_half = [const.tile([P, 4, HID // 2], BF16, name="c0_%d" % half) for half in range(2)]
+        raw = {}
 
         def load_bias(q):
             for s in range(2):
@@ -77,30 +93,26 @@ def tile_lstmcell_kernel(
                     in_=biases[q][s].rearrange("(j p) -> j p", p=P),
                 )
 
-        c0_half = [const.tile([P, 4, HID // 2], BF16, name="c0_%d" % half) for half in range(2)]
-        raw = {}
-
         def load_x(s):
             view = (x, h0)[s].rearrange("(p t) k -> p t k", t=4)
             for th in range(2):
                 t = raw_pool.tile([P, 2 * K], BF16, name="x%d_%d" % (s, th), tag="raw")
-                nc.sync.dma_start(
-                    out=t[:].rearrange("p (t k) -> p t k", t=2), in_=view[:, 2 * th:2 * th + 2, :],
-                )
+                for tt in range(2):
+                    nc.sync.dma_start(out=t[:, tt * K:(tt + 1) * K], in_=view[:, 2 * th + tt, :])
                 raw[("x", s, th)] = t
 
-        def load_w(j, pair, s):
-            t = raw_pool.tile([P, 2 * K], BF16, name="w%d_%d_%d" % (j, pair, s), tag="raw")
-            for hh in range(2):
-                nc.sync.dma_start(
-                    out=t[:, hh * K:(hh + 1) * K], in_=weights[2 * pair + hh][s][j * P:(j + 1) * P, :],
-                )
-            raw[(j, pair, s)] = t
+        def load_w(r, s):
+            t = raw_pool.tile([P, 2 * K], BF16, name="w%d_%d" % (r, s), tag="raw")
+            for hh, (q, j) in enumerate(parts_of(r)):
+                nc.sync.dma_start(out=t[:, hh * K:(hh + 1) * K], in_=weights[q][s][j * P:(j + 1) * P, :])
+            raw[(r, s)] = t
 
         def load_round(r):
-            j, pair = divmod(r, 2)
             for s in range(2):
-                load_w(j, pair, s)
+                load_w(r, s)
+            if r == BIAS_O_AFTER:
+                for s in range(2):
+                    nc.sync.dma_start(out=orow[s:s + 1, :], in_=biases[3][s].rearrange("(u h) -> u h", u=1))
             if r in C0_AFTER:
                 half = C0_AFTER.index(r)
                 nc.sync.dma_start(
@@ -108,12 +120,12 @@ def tile_lstmcell_kernel(
                     in_=c0.rearrange("(p t) h -> p t h", t=4)[:, :, half * (HID // 2):(half + 1) * (HID // 2)],
                 )
 
-        for q in range(4):
+        for q in range(3):
             load_bias(q)
         for s in range(2):
             load_x(s)
-            for pair in range(2):
-                load_w(0, pair, s)
+            for r in range(2):
+                load_w(r, s)
         for r in range(2, AHEAD):
             load_round(r)
 
@@ -125,8 +137,14 @@ def tile_lstmcell_kernel(
         xq = const.tile([P, 4 * 512], U32, name="xq", align_bytes=64)
         xs = const.tile([P, 4 * 512], U8, name="xs", align_bytes=64)
 
+        def is_moving(key):
+            return key[0] != "x" and key[0] % 4 == 3
+
+        def label(key):
+            return "_".join([str(k) for k in key])
+
         def reorder(key, parts=1):
-            t = perm_pool.tile([P, 2 * K], BF16, name="p%s_%d_%d" % key, tag="perm")
+            t = perm_pool.tile([P, 2 * K], BF16, name="p" + label(key), tag="perm")
             n = 2 * K // parts
             for part in range(parts):
                 cs = slice(part * n, (part + 1) * n)
@@ -140,22 +158,35 @@ def tile_lstmcell_kernel(
             step = 1 if key in perm else 2
             src = (perm if key in perm else raw)[key][:].bitcast(F32)
             for b in range(2):
-                bank = tr_pool.tile([P, 512], F32, name="tr%s_%d_%d_%d" % (key + (b,)), tag="tr")
+                bank = tr_pool.tile([P, 512], F32, name="tr%s_%d" % (label(key), b), tag="tr")
                 for i in range(4):
-                    c = 512 * (i // 2) + 256 * b if key[0] == "x" else 512 * b + 256 * (i // 2)
+                    c = 512 * (i // 2) + 256 * b if is_moving(key) else 512 * b + 256 * (i // 2)
                     c += (i % 2) * (P if step == 1 else 1)
                     nc.tensor.transpose(
                         bank[:, i * P:(i + 1) * P], src[:, c:c + step * (P - 1) + 1:step], ident[:],
                     )
                 tr_banks[key + (b,)] = bank
 
+        def evacuate_x(key, b, on_scalar):
+            for g in range(2):
+                gkey = ("x", key[1], g)
+                if gkey not in grp:
+                    grp[gkey] = grp_pool.tile([P, 2048], BF16, name="g" + label(gkey), tag="grp", align_bytes=64)
+                t = 2 * key[2] + b
+                src = tr_banks[key + (b,)][:, g * 256:(g + 1) * 256].rearrange("p (u c) -> p c u", u=2)
+                dst = grp[gkey][:, t * 512:(t + 1) * 512].bitcast(F32).rearrange("p (c u) -> p c u", u=2)
+                if on_scalar:
+                    nc.scalar.copy(out=dst, in_=src)
+                else:
+                    nc.vector.tensor_copy(out=dst, in_=src)
+
         def evacuate(key, b, on_scalar=True):
             if key[0] == "x":
-                gkey, half = ("x", key[1], b), key[2]
-            else:
-                gkey, half = key, b
+                evacuate_x(key, b, on_scalar)
+                return
+            gkey, half = key, b
             if gkey not in grp:
-                grp[gkey] = grp_pool.tile([P, 2048], BF16, name="g%s_%d_%d" % gkey, tag="grp", align_bytes=64)
+                grp[gkey] = grp_pool.tile([P, 2048], BF16, name="g" + label(gkey), tag="grp", align_bytes=64)
             src = tr_banks[key + (b,)][:].rearrange("p (a u c) -> p a c u", a=2, u=2)
             dst = grp[gkey][:, half * 1024:(half + 1) * 1024].bitcast(F32).rearrange("p (a c u) -> p a c u", a=2, u=2)
             if on_scalar:
@@ -170,36 +201,53 @@ def tile_lstmcell_kernel(
             )
 
         def quant(key):
-            wq[key] = code_pool.tile([P, 512], U32, name="wq%d_%d_%d" % key, tag="wq", align_bytes=64)
-            ws[key] = code_pool.tile([P, 512], U8, name="ws%d_%d_%d" % key, tag="ws", align_bytes=64)
+            wq[key] = code_pool.tile([P, 512], U32, name="wq" + label(key), tag="wq", align_bytes=64)
+            ws[key] = code_pool.tile([P, 512], U8, name="ws" + label(key), tag="ws", align_bytes=64)
             nc.vector.quantize_mx(out=wq[key][:].bitcast(FP8X4), scales=ws[key][:], in_=grp[key][:])
 
         accs = {}
         gate = {}
         prod = {}
         banks = {}
-        outs = {}
-        tanh_c = {}
+        pair_c = {}
+        pair_h = {}
+        pair_o = {}
+        pair_th = {}
 
-        def mx(j, q, s):
-            key = (j, q // 2, s)
+        def mx(r, hh, s):
             if s == 0:
-                pool, tag = (back_pool, "back") if j == 0 and q >= 2 else (acc_pool, "acc")
-                accs[(j, q)] = pool.tile([P, 512], F32, name="acc%d_%d" % (j, q), tag=tag)
+                pool, tag = (back_pool, "back") if r == 1 else (acc_pool, "acc")
+                accs[(r, hh)] = pool.tile([P, 512], F32, name="acc%d_%d" % (r, hh), tag=tag)
             for g in range(2):
-                wc = (q % 2) * 256 + g * 128
+                wc = hh * 256 + g * 128
                 xc = (2 * s + g) * 512
                 nc.tensor.matmul_mx(
-                    out=accs[(j, q)][:],
-                    lhsT=wq[key][:, wc:wc + 128].bitcast(FP8X4), lhsT_scale=ws[key][:, wc:wc + 128],
+                    out=accs[(r, hh)][:],
+                    lhsT=wq[(r, s)][:, wc:wc + 128].bitcast(FP8X4), lhsT_scale=ws[(r, s)][:, wc:wc + 128],
                     rhs=xq[:, xc:xc + 512].bitcast(FP8X4), rhs_scale=xs[:, xc:xc + 512],
                     start=(s == 0 and g == 0), stop=(s == 1 and g == 1),
                 )
 
-        def act(j, q):
+        def mx_o(r, half, pool=acc_pool, tag="acc"):
+            acc = pool.tile([P, 512], F32, name="acc%d_%d" % (r, half), tag=tag)
+            for tt in range(2):
+                for s in range(2):
+                    for g in range(2):
+                        xc = (2 * s + g) * 512 + (2 * half + tt) * P
+                        nc.tensor.matmul_mx(
+                            out=acc[:, tt * 256:(tt + 1) * 256],
+                            lhsT=xq[:, xc:xc + P].bitcast(FP8X4), lhsT_scale=xs[:, xc:xc + P],
+                            rhs=wq[(r, s)][:, g * 256:(g + 1) * 256].bitcast(FP8X4),
+                            rhs_scale=ws[(r, s)][:, g * 256:(g + 1) * 256],
+                            start=(s == 0 and g == 0), stop=(s == 1 and g == 1),
+                        )
+            accs[(r, half)] = acc[:].rearrange("p (t h) -> p t h", t=2)
+
+        def act(r, hh):
+            q, j = parts_of(r)[hh]
             a = act_pool.tile([P, 512], F32, name="gate%d_%d" % (j, q), tag="gate%d" % q)
             nc.scalar.activation(
-                out=a[:], in_=accs[(j, q)][:], func=funcs[q], bias=bias_sb[:, 8 * q + j:8 * q + j + 1], scale=1.0,
+                out=a[:], in_=accs[(r, hh)][:], func=funcs[q], bias=bias_sb[:, 8 * q + j:8 * q + j + 1], scale=1.0,
             )
             gate[(j, q)] = a
 
@@ -208,47 +256,61 @@ def tile_lstmcell_kernel(
             nc.vector.tensor_tensor(out=t[:], in0=gate[(j, 0)][:], in1=gate[(j, 1)][:], op=ALU.mult)
             prod[j] = t
 
-        def tr_out(j, what, pool=back_pool, tag="back"):
-            src = {"f": gate.get((j, 2)), "u": prod.get(j), "o": gate.get((j, 3))}[what]
-            bank = pool.tile([P, 512], F32, name="ob%s%d" % (what, j), tag=tag)
+        def tr_out(j, what):
+            src = gate[(j, 2)] if what == "f" else prod[j]
+            bank = back_pool.tile([P, 512], F32, name="ob%s%d" % (what, j), tag="back")
             for t in range(4):
                 nc.tensor.transpose(bank[:, t * P:(t + 1) * P], src[:, t * P:(t + 1) * P], ident[:])
             banks[(j, what)] = bank[:].rearrange("p (t h) -> p t h", t=4)
 
-        def group_of(j):
-            return [js for js in STORE_GROUPS if j in js][0]
-
-        def cell(j):
-            js = group_of(j)
-            width = P * len(js)
-            if j == js[0]:
-                outs[js] = (
-                    out_pool.tile([P, 4, width], F32, name="oh%d" % j, tag="oh"),
-                    out_pool.tile([P, 4, width], F32, name="oc%d" % j, tag="oc"),
-                )
-            off = (j - js[0]) * P
+        def cell(j, parts=1):
+            m, e = divmod(j, 2)
+            if e == 0:
+                pair_c[m] = out_pool.tile([P, 4, 256], F32, name="oc%d" % m, tag="oc")
+                pair_th[m] = ep_pool.tile([P, 4, 256], F32, name="th%d" % m, tag="th")
+            cols = slice(e * P, (e + 1) * P)
             t1 = ep_pool.tile([P, 4, P], F32, name="t1_%d" % j, tag="t1")
-            nc.vector.tensor_tensor(
-                out=t1[:], in0=banks[(j, "f")], in1=c0_half[j // 4][:, :, (j % 4) * P:(j % 4 + 1) * P], op=ALU.mult,
-            )
-            nc.vector.tensor_tensor(out=outs[js][1][:, :, off:off + P], in0=banks[(j, "u")], in1=t1[:], op=ALU.add)
-            if j == js[-1]:
-                nc.sync.dma_start(out=out_c[:, :, js[0] * P:(js[-1] + 1) * P], in_=outs[js][1][:])
+            n = 4 // parts
+            for part in range(parts):
+                ts = slice(part * n, (part + 1) * n)
+                nc.vector.tensor_tensor(
+                    out=t1[:, ts, :], in0=banks[(j, "f")][:, ts, :], in1=c0_half[j // 4][:, ts, (j % 4) * P:(j % 4 + 1) * P], op=ALU.mult,
+                )
+                nc.vector.tensor_tensor(
+                    out=pair_c[m][:, ts, cols], in0=banks[(j, "u")][:, ts, :], in1=t1[:, ts, :], op=ALU.add,
+                )
+            if e == 1:
+                nc.sync.dma_start(out=out_c[:, :, m * 256:(m + 1) * 256], in_=pair_c[m][:])
 
-        def tanh_cell(j):
-            js = group_of(j)
-            off = (j - js[0]) * P
-            tanh_c[j] = ep_pool.tile([P, 4, P], F32, name="th%d" % j, tag="th")
-            nc.scalar.activation(out=tanh_c[j][:], in_=outs[js][1][:, :, off:off + P], func=ACT.Tanh)
+        def tanh_cell(j, parts=1):
+            m, e = divmod(j, 2)
+            cols = slice(e * P, (e + 1) * P)
+            n = 4 // parts
+            for part in range(parts):
+                ts = slice(part * n, (part + 1) * n)
+                nc.scalar.activation(out=pair_th[m][:, ts, cols], in_=pair_c[m][:, ts, cols], func=ACT.Tanh)
 
-        def hidden(j):
-            js = group_of(j)
-            off = (j - js[0]) * P
+        def add_bias_o(m, half):
+            pair_o[(m, half)] = act_pool.tile([P, 2, 256], F32, name="o%d_%d" % (m, half), tag="o%d" % half)
             nc.vector.tensor_tensor(
-                out=outs[js][0][:, :, off:off + P], in0=banks[(j, "o")], in1=tanh_c[j][:], op=ALU.mult,
+                out=pair_o[(m, half)][:], in0=accs[(4 * m + 3, half)],
+                in1=bias_o[:, m * 256:(m + 1) * 256].unsqueeze(1).to_broadcast([P, 2, 256]), op=ALU.add,
             )
-            if j == js[-1]:
-                nc.sync.dma_start(out=out_h[:, :, js[0] * P:(js[-1] + 1) * P], in_=outs[js][0][:])
+
+        def sigmoid_o(m, half):
+            o = pair_o[(m, half)]
+            nc.scalar.activation(out=o[:], in_=o[:], func=ACT.Sigmoid)
+
+        def hidden(m, half):
+            ts = slice(2 * half, 2 * half + 2)
+            if half == 0:
+                pair_h[m] = out_pool.tile([P, 4, 256], F32, name="oh%d" % m, tag="oh")
+            nc.vector.tensor_tensor(
+                out=pair_h[m][:, ts, :], in0=pair_o[(m, half)][:], in1=pair_th[m][:, ts, :], op=ALU.mult,
+            )
+            if half == 1 or m == NM - 1:
+                hs = ts if m == NM - 1 else slice(0, 4)
+                nc.sync.dma_start(out=out_h[:, hs, m * 256:(m + 1) * 256], in_=pair_h[m][:, hs, :])
 
         def do_x(s, th, share):
             key = ("x", s, th)
@@ -256,156 +318,133 @@ def tile_lstmcell_kernel(
             evacuate(key, 0)
             evacuate(key, 1, on_scalar=not share)
 
-        def do_w(key):
+        def do_w(key, share=False):
             transpose(key)
-            for b in range(2):
-                evacuate(key, b)
+            evacuate(key, 0)
+            evacuate(key, 1, on_scalar=not share)
 
         keep_clock(10, "idle_start")
         do_x(0, 0, True)
         keep_clock(1, "idle_a")
         do_x(0, 1, True)
         keep_clock(1, "idle_b")
-        do_w((0, 0, 0))
+        do_w((0, 0))
         quant_x(0, 0)
         quant_x(0, 1)
-        do_w((0, 1, 0))
-        quant((0, 0, 0))
+        do_w((1, 0))
+        quant((0, 0))
         do_x(1, 0, False)
-        quant((0, 1, 0))
-        for q in range(2):
-            mx(0, q, 0)
+        quant((1, 0))
+        for hh in range(2):
+            mx(0, hh, 0)
         do_x(1, 1, False)
-        reorder((0, 0, 1), 2)
-        do_w((0, 0, 1))
-        reorder((0, 1, 1), 2)
-        for q in range(2, 4):
-            mx(0, q, 0)
+        reorder((0, 1), 2)
+        do_w((0, 1))
+        reorder((1, 1), 2)
+        for hh in range(2):
+            mx(1, hh, 0)
         quant_x(1, 0)
         quant_x(1, 1)
 
         bsum = const.tile([P, P], F32, name="bsum")
         nc.vector.tensor_tensor(out=bsum[:], in0=braw[:, 0:P], in1=braw[:, P:2 * P], op=ALU.add)
-        do_w((0, 1, 1))
-        reorder((1, 0, 0), 2)
-        quant((0, 0, 1))
+        do_w((1, 1))
+        quant((0, 1))
+        reorder((2, 0), 2)
         pb = tr_pool.tile([P, 512], F32, name="pb", tag="tr")
         nc.tensor.transpose(pb[:, 0:P], bsum[:], ident[:])
         bias_sb = const.tile([P, 32], F32, name="bias_sb")
         nc.vector.tensor_copy(out=bias_sb[:], in_=pb[:, 0:32])
+        bias_o = const.tile([P, HID], F32, name="bias_o")
 
-        for r in range(NR - 2):
-            j, pair = divmod(r, 2)
-            for s in range(1 if r == 0 else 0, 2):
-                reorder(divmod(r + 2, 2) + (s,))
-            if r > 0:
+        for r in range(NR):
+            m, kind = divmod(r, 4)
+            a, b = 2 * m, 2 * m + 1
+            if r + 2 < NR:
+                for s in range(1 if r == 0 else 0, 2):
+                    reorder((r + 2, s))
+                    if s == 0 and kind == 0 and m > 0:
+                        add_bias_o(m - 1, 1)
+            if 0 < r < NR - 1:
                 for s in range(2):
-                    do_w(divmod(r + 1, 2) + (s,))
-            if pair == 0:
-                if j > 0:
-                    tr_out(j - 1, "f")
-                    tr_out(j - 1, "u")
-                    cell(j - 1)
-                    tanh_cell(j - 1)
-            else:
-                if j > 0:
-                    tr_out(j - 1, "o")
-                    hidden(j - 1)
-                mul_ig(j)
-            for s in range(1 if r == 0 else 0, 2):
-                quant(divmod(r + 1, 2) + (s,))
-            for q in (2 * pair, 2 * pair + 1):
-                if r > 1:
-                    mx(j, q, 0)
-                mx(j, q, 1)
-                act(j, q)
+                    do_w((r + 1, s))
+            if kind == 0 and m > 0:
+                tr_out(b - 2, "u")
+                sigmoid_o(m - 1, 0)
+                cell(b - 2)
+            elif kind == 1:
+                mul_ig(a)
+                if m > 0:
+                    tanh_cell(b - 2)
+            elif kind == 2:
+                tr_out(a, "f")
+                tr_out(a, "u")
+                if m > 0:
+                    hidden(m - 1, 0)
+                if m == NM - 1:
+                    hidden(m - 1, 1)
+                cell(a)
+                if 0 < m < NM - 1:
+                    sigmoid_o(m - 1, 1)
+            elif kind == 3:
+                tr_out(b, "f")
+                mul_ig(b)
+                tanh_cell(a)
+            if r + 1 < NR:
+                for s in range(1 if r == 0 else 0, 2):
+                    quant((r + 1, s))
+            if kind == 3 and 0 < m < NM - 1:
+                hidden(m - 1, 1)
+            if kind < 3:
+                for hh in range(2):
+                    if r > 1:
+                        mx(r, hh, 0)
+                    mx(r, hh, 1)
+                    act(r, hh)
+                if r == NR - 3:
+                    sigmoid_o(m - 1, 1)
+            elif r + 1 < NR:
+                for half in range(2):
+                    mx_o(r, half)
+                add_bias_o(m, 0)
+            if r in (2, 6):
+                cs = slice(r // 4 * 512, r // 4 * 512 + 512)
+                bank = tr_pool.tile([P, 512], F32, name="bo%d" % r, tag="tr")
+                nc.tensor.matmul(out=bank[:], lhsT=ones[:], rhs=orow[:, cs], start=True, stop=True)
+                nc.vector.tensor_copy(out=bias_o[:, cs], in_=bank[:])
             if r + AHEAD < NR:
                 load_round(r + AHEAD)
 
-        j = NT - 1
-        cols = slice(j * P, (j + 1) * P)
-        part = {}
-
-        def half_gate(half, q, pool, tag):
-            acc = pool.tile([P, 512], F32, name="accl%d_%d" % (half, q), tag=tag)
-            for s in range(2):
-                key = (j, q // 2, s)
-                for g in range(2):
-                    wc = (q % 2) * 256 + g * 128
-                    xc = (2 * s + g) * 512 + half * 256
-                    nc.tensor.matmul_mx(
-                        out=acc[:, 0:256],
-                        lhsT=wq[key][:, wc:wc + 128].bitcast(FP8X4), lhsT_scale=ws[key][:, wc:wc + 128],
-                        rhs=xq[:, xc:xc + 256].bitcast(FP8X4), rhs_scale=xs[:, xc:xc + 256],
-                        start=(s == 0 and g == 0), stop=(s == 1 and g == 1),
-                    )
-            a = last_pool.tile([P, 256], F32, name="gatel%d_%d" % (half, q), tag="g%d" % q)
-            nc.scalar.activation(
-                out=a[:], in_=acc[:, 0:256], func=funcs[q], bias=bias_sb[:, 8 * q + j:8 * q + j + 1], scale=1.0,
-            )
-            part[(half, q)] = a
-
-        def half_ig(half):
-            part[(half, "u")] = last_pool.tile([P, 256], F32, name="igl%d" % half, tag="u")
-            nc.vector.tensor_tensor(
-                out=part[(half, "u")][:], in0=part[(half, 0)][:], in1=part[(half, 1)][:], op=ALU.mult,
-            )
-
-        def half_out(half, what, pool, tag):
-            bank = pool.tile([P, 512], F32, name="obl%d_%s" % (half, what), tag=tag)
-            for t in range(2):
-                nc.tensor.transpose(bank[:, t * P:(t + 1) * P], part[(half, what)][:, t * P:(t + 1) * P], ident[:])
-            banks[(half, what)] = bank[:, 0:256].rearrange("p (t h) -> p t h", t=2)
-
-        def half_cell(half):
+        m, j = NM - 1, NT - 1
+        cols = slice(m * 256, (m + 1) * 256)
+        late = slice(P, 2 * P)
+        mx_o(NR - 1, 0, tr_pool, "tr")
+        tr_out(j, "u")
+        mx_o(NR - 1, 1, tr_pool, "tr")
+        t1 = ep_pool.tile([P, 4, P], F32, name="t1_%d" % j, tag="t1")
+        nc.vector.tensor_tensor(
+            out=t1[:], in0=banks[(j, "f")], in1=c0_half[1][:, :, HID // 2 - P:HID // 2], op=ALU.mult,
+        )
+        add_bias_o(m, 0)
+        sigmoid_o(m, 0)
+        for half in range(2):
             ts = slice(2 * half, 2 * half + 2)
-            t1 = last_pool.tile([P, 2, P], F32, name="t1l%d" % half, tag="t1")
-            c = last_pool.tile([P, 2, P], F32, name="cl%d" % half, tag="c")
             nc.vector.tensor_tensor(
-                out=t1[:], in0=banks[(half, 2)], in1=c0_half[1][:, ts, HID // 2 - P:HID // 2], op=ALU.mult,
+                out=pair_c[m][:, ts, late], in0=banks[(j, "u")][:, ts, :], in1=t1[:, ts, :], op=ALU.add,
             )
-            nc.vector.tensor_tensor(out=c[:], in0=banks[(half, "u")], in1=t1[:], op=ALU.add)
-            nc.sync.dma_start(out=out_c[:, ts, cols], in_=c[:])
-            part[(half, "c")] = c
-
-        def half_tanh(half):
-            part[(half, "th")] = last_pool.tile([P, 2, P], F32, name="thl%d" % half, tag="th")
-            nc.scalar.activation(out=part[(half, "th")][:], in_=part[(half, "c")][:], func=ACT.Tanh)
-
-        def half_hidden(half):
-            h = last_pool.tile([P, 2, P], F32, name="hl%d" % half, tag="h")
-            nc.vector.tensor_tensor(out=h[:], in0=banks[(half, 3)], in1=part[(half, "th")][:], op=ALU.mult)
-            nc.sync.dma_start(out=out_h[:, 2 * half:2 * half + 2, cols], in_=h[:])
-
-        for s in range(2):
-            do_w((j, 1, s))
-        tr_out(j - 1, "f")
-        tr_out(j - 1, "u")
-        cell(j - 1)
-        tr_out(j - 1, "o", tr_pool, "tr")
-        for s in range(2):
-            quant((j, 1, s))
-        half_gate(0, 0, acc_pool, "acc")
-        half_gate(0, 1, acc_pool, "acc")
-        tanh_cell(j - 1)
-        half_ig(0)
-        hidden(j - 1)
-        half_gate(1, 0, back_pool, "back")
-        half_gate(1, 1, back_pool, "back")
-        half_ig(1)
-        half_gate(0, 2, tr_pool, "tr")
-        half_gate(0, 3, tr_pool, "tr")
-        half_gate(1, 2, tr_pool, "tr")
-        half_out(0, 2, acc_pool, "acc")
-        half_out(0, "u", acc_pool, "acc")
-        half_cell(0)
-        half_tanh(0)
-        half_out(0, 3, tr_pool, "tr")
-        half_out(1, "u", tr_pool, "tr")
-        half_out(1, 2, tr_pool, "tr")
-        half_cell(1)
-        half_gate(1, 3, tr_pool, "tr")
-        half_hidden(0)
-        half_tanh(1)
-        half_out(1, 3, back_pool, "back")
-        half_hidden(1)
+            nc.scalar.activation(out=pair_th[m][:, ts, late], in_=pair_c[m][:, ts, late], func=ACT.Tanh)
+        nc.sync.dma_start(out=out_c[:, :, cols], in_=pair_c[m][:])
+        pair_o[(m, 1)] = act_pool.tile([P, 2, 256], F32, name="o%d_1" % m, tag="o1")
+        o1 = pair_o[(m, 1)]
+        for tt in range(2):
+            nc.vector.tensor_tensor(
+                out=o1[:, tt, :], in0=accs[(NR - 1, 1)][:, tt, :], in1=bias_o[:, cols], op=ALU.add,
+            )
+            nc.scalar.activation(out=o1[:, tt, :], in_=o1[:, tt, :], func=ACT.Sigmoid)
+        hidden(m, 0)
+        for tt in range(2):
+            t = 2 + tt
+            nc.vector.tensor_tensor(
+                out=pair_h[m][:, t, :], in0=o1[:, tt, :], in1=pair_th[m][:, t, :], op=ALU.mult,
+            )
+            nc.sync.dma_start(out=out_h[:, t, cols], in_=pair_h[m][:, t, :])

from contextlib import ExitStack

import concourse.mybir as mybir
from concourse.masks import make_identity

F32 = mybir.dt.float32
BF16 = mybir.dt.bfloat16
U32 = mybir.dt.uint32
U8 = mybir.dt.uint8
FP8X4 = mybir.dt.float8_e4m3fn_x4
ACT = mybir.ActivationFunctionType
ALU = mybir.AluOpType

P = 128
BATCH = 512
K = 1024
HID = 1024
FLOPS = 2 * BATCH * (2 * K) * (4 * HID)

NT = HID // P
NM = NT // 2
NR = 4 * NM
AHEAD = 8
C0_AFTER = (3, 7)
BIAS_O_AFTER = 4


def tile_lstmcell_kernel(
    tc, x, h0, c0,
    W_ii, b_ii, W_hi, b_hi,
    W_if, b_if, W_hf, b_hf,
    W_ig, b_ig, W_hg, b_hg,
    W_io, b_io, W_ho, b_ho,
    out_0, out_1,
):
    nc = tc.nc
    weights = ((W_ii, W_hi), (W_ig, W_hg), (W_if, W_hf), (W_io, W_ho))
    biases = ((b_ii, b_hi), (b_ig, b_hg), (b_if, b_hf), (b_io, b_ho))
    funcs = (ACT.Sigmoid, ACT.Tanh, ACT.Sigmoid, ACT.Sigmoid)
    out_h = out_0.rearrange("(p t) h -> p t h", t=4)
    out_c = out_1.rearrange("(p t) h -> p t h", t=4)

    def parts_of(r):
        m, kind = divmod(r, 4)
        if kind == 0:
            return ((0, 2 * m), (1, 2 * m))
        if kind == 1:
            return ((2, 2 * m), (2, 2 * m + 1))
        if kind == 2:
            return ((0, 2 * m + 1), (1, 2 * m + 1))
        return ((3, 2 * m), (3, 2 * m + 1))

    with ExitStack() as ctx:
        const = ctx.enter_context(tc.tile_pool(name="const", bufs=1))
        raw_pool = ctx.enter_context(tc.tile_pool(name="raw", bufs=2 * AHEAD + 4))
        perm_pool = ctx.enter_context(tc.tile_pool(name="perm", bufs=5))
        grp_pool = ctx.enter_context(tc.tile_pool(name="grp", bufs=6))
        code_pool = ctx.enter_context(tc.tile_pool(name="code", bufs=6))
        act_pool = ctx.enter_context(tc.tile_pool(name="act", bufs=3))
        ep_pool = ctx.enter_context(tc.tile_pool(name="ep", bufs=2))
        out_pool = ctx.enter_context(tc.tile_pool(name="outp", bufs=2))
        acc_pool = ctx.enter_context(tc.psum_pool(name="acc", bufs=2))
        back_pool = ctx.enter_context(tc.psum_pool(name="back", bufs=2))
        tr_pool = ctx.enter_context(tc.psum_pool(name="tr", bufs=4))
        ctx.enter_context(tc.manual_schedule())

        zeros = const.tile([P, 512], BF16, name="zeros")
        nc.vector.memset(zeros[:], 0.0)
        warm = const.tile([P, 1], F32, name="warm")
        nc.vector.memset(warm[:], 0.0)
        braw = const.tile([P, 2 * P], BF16, name="braw")
        nc.vector.memset(braw[:], 0.0)
        ident = const.tile([P, P], F32, name="ident")
        make_identity(nc, ident[:])
        ones = const.tile([P, P], BF16, name="ones")
        nc.gpsimd.memset(ones[:], 1.0)
        orow = const.tile([P, HID], BF16, name="orow")
        nc.gpsimd.memset(orow[:], 0.0)

        def keep_clock(n, name):
            idle = acc_pool.tile([P, 512], F32, name=name, tag="acc")
            for i in range(n):
                nc.tensor.matmul(out=idle[:], lhsT=zeros[:, 0:P], rhs=zeros[:], start=True, stop=True)

        nc.scalar.activation(out=warm[:], in_=warm[:], func=ACT.Sigmoid)
        c0_half = [const.tile([P, 4, HID // 2], BF16, name="c0_%d" % half) for half in range(2)]
        raw = {}

        def load_bias(q):
            for s in range(2):
                nc.gpsimd.dma_start(
                    out=braw[8 * q:8 * q + 8, s * P:(s + 1) * P],
                    in_=biases[q][s].rearrange("(j p) -> j p", p=P),
                )

        def load_x(s):
            view = (x, h0)[s].rearrange("(p t) k -> p t k", t=4)
            for th in range(2):
                t = raw_pool.tile([P, 2 * K], BF16, name="x%d_%d" % (s, th), tag="raw")
                for tt in range(2):
                    nc.sync.dma_start(out=t[:, tt * K:(tt + 1) * K], in_=view[:, 2 * th + tt, :])
                raw[("x", s, th)] = t

        def load_w(r, s):
            t = raw_pool.tile([P, 2 * K], BF16, name="w%d_%d" % (r, s), tag="raw")
            for hh, (q, j) in enumerate(parts_of(r)):
                nc.sync.dma_start(out=t[:, hh * K:(hh + 1) * K], in_=weights[q][s][j * P:(j + 1) * P, :])
            raw[(r, s)] = t

        def load_round(r):
            for s in range(2):
                load_w(r, s)
            if r == BIAS_O_AFTER:
                for s in range(2):
                    nc.sync.dma_start(out=orow[s:s + 1, :], in_=biases[3][s].rearrange("(u h) -> u h", u=1))
            if r in C0_AFTER:
                half = C0_AFTER.index(r)
                nc.sync.dma_start(
                    out=c0_half[half][:],
                    in_=c0.rearrange("(p t) h -> p t h", t=4)[:, :, half * (HID // 2):(half + 1) * (HID // 2)],
                )

        for q in range(3):
            load_bias(q)
        for s in range(2):
            load_x(s)
            for r in range(2):
                load_w(r, s)
        for r in range(2, AHEAD):
            load_round(r)

        perm = {}
        tr_banks = {}
        grp = {}
        wq = {}
        ws = {}
        xq = const.tile([P, 4 * 512], U32, name="xq", align_bytes=64)
        xs = const.tile([P, 4 * 512], U8, name="xs", align_bytes=64)

        def is_moving(key):
            return key[0] != "x" and key[0] % 4 == 3

        def label(key):
            return "_".join([str(k) for k in key])

        def reorder(key, parts=1):
            t = perm_pool.tile([P, 2 * K], BF16, name="p" + label(key), tag="perm")
            n = 2 * K // parts
            for part in range(parts):
                cs = slice(part * n, (part + 1) * n)
                nc.vector.tensor_copy(
                    out=t[:, cs].bitcast(F32).rearrange("p (g u b i) -> p g b u i", u=2, b=32, i=4),
                    in_=raw[key][:, cs].bitcast(F32).rearrange("p (g b i u) -> p g b u i", u=2, b=32, i=4),
                )
            perm[key] = t

        def transpose(key):
            step = 1 if key in perm else 2
            src = (perm if key in perm else raw)[key][:].bitcast(F32)
            for b in range(2):
                bank = tr_pool.tile([P, 512], F32, name="tr%s_%d" % (label(key), b), tag="tr")
                for i in range(4):
                    c = 512 * (i // 2) + 256 * b if is_moving(key) else 512 * b + 256 * (i // 2)
                    c += (i % 2) * (P if step == 1 else 1)
                    nc.tensor.transpose(
                        bank[:, i * P:(i + 1) * P], src[:, c:c + step * (P - 1) + 1:step], ident[:],
                    )
                tr_banks[key + (b,)] = bank

        def evacuate_x(key, b, on_scalar):
            for g in range(2):
                gkey = ("x", key[1], g)
                if gkey not in grp:
                    grp[gkey] = grp_pool.tile([P, 2048], BF16, name="g" + label(gkey), tag="grp", align_bytes=64)
                t = 2 * key[2] + b
                src = tr_banks[key + (b,)][:, g * 256:(g + 1) * 256].rearrange("p (u c) -> p c u", u=2)
                dst = grp[gkey][:, t * 512:(t + 1) * 512].bitcast(F32).rearrange("p (c u) -> p c u", u=2)
                if on_scalar:
                    nc.scalar.copy(out=dst, in_=src)
                else:
                    nc.vector.tensor_copy(out=dst, in_=src)

        def evacuate(key, b, on_scalar=True):
            if key[0] == "x":
                evacuate_x(key, b, on_scalar)
                return
            gkey, half = key, b
            if gkey not in grp:
                grp[gkey] = grp_pool.tile([P, 2048], BF16, name="g" + label(gkey), tag="grp", align_bytes=64)
            src = tr_banks[key + (b,)][:].rearrange("p (a u c) -> p a c u", a=2, u=2)
            dst = grp[gkey][:, half * 1024:(half + 1) * 1024].bitcast(F32).rearrange("p (a c u) -> p a c u", a=2, u=2)
            if on_scalar:
                nc.scalar.copy(out=dst, in_=src)
            else:
                nc.vector.tensor_copy(out=dst, in_=src)

        def quant_x(s, g):
            c = (2 * s + g) * 512
            nc.vector.quantize_mx(
                out=xq[:, c:c + 512].bitcast(FP8X4), scales=xs[:, c:c + 512], in_=grp[("x", s, g)][:],
            )

        def quant(key):
            wq[key] = code_pool.tile([P, 512], U32, name="wq" + label(key), tag="wq", align_bytes=64)
            ws[key] = code_pool.tile([P, 512], U8, name="ws" + label(key), tag="ws", align_bytes=64)
            nc.vector.quantize_mx(out=wq[key][:].bitcast(FP8X4), scales=ws[key][:], in_=grp[key][:])

        accs = {}
        gate = {}
        prod = {}
        banks = {}
        pair_c = {}
        pair_h = {}
        pair_o = {}
        pair_th = {}

        def mx(r, hh, s):
            if s == 0:
                pool, tag = (back_pool, "back") if r == 1 else (acc_pool, "acc")
                accs[(r, hh)] = pool.tile([P, 512], F32, name="acc%d_%d" % (r, hh), tag=tag)
            for g in range(2):
                wc = hh * 256 + g * 128
                xc = (2 * s + g) * 512
                nc.tensor.matmul_mx(
                    out=accs[(r, hh)][:],
                    lhsT=wq[(r, s)][:, wc:wc + 128].bitcast(FP8X4), lhsT_scale=ws[(r, s)][:, wc:wc + 128],
                    rhs=xq[:, xc:xc + 512].bitcast(FP8X4), rhs_scale=xs[:, xc:xc + 512],
                    start=(s == 0 and g == 0), stop=(s == 1 and g == 1),
                )

        def mx_o(r, half, pool=acc_pool, tag="acc"):
            acc = pool.tile([P, 512], F32, name="acc%d_%d" % (r, half), tag=tag)
            for tt in range(2):
                for s in range(2):
                    for g in range(2):
                        xc = (2 * s + g) * 512 + (2 * half + tt) * P
                        nc.tensor.matmul_mx(
                            out=acc[:, tt * 256:(tt + 1) * 256],
                            lhsT=xq[:, xc:xc + P].bitcast(FP8X4), lhsT_scale=xs[:, xc:xc + P],
                            rhs=wq[(r, s)][:, g * 256:(g + 1) * 256].bitcast(FP8X4),
                            rhs_scale=ws[(r, s)][:, g * 256:(g + 1) * 256],
                            start=(s == 0 and g == 0), stop=(s == 1 and g == 1),
                        )
            accs[(r, half)] = acc[:].rearrange("p (t h) -> p t h", t=2)

        def act(r, hh):
            q, j = parts_of(r)[hh]
            a = act_pool.tile([P, 512], F32, name="gate%d_%d" % (j, q), tag="gate%d" % q)
            nc.scalar.activation(
                out=a[:], in_=accs[(r, hh)][:], func=funcs[q], bias=bias_sb[:, 8 * q + j:8 * q + j + 1], scale=1.0,
            )
            gate[(j, q)] = a

        def mul_ig(j):
            t = act_pool.tile([P, 512], F32, name="ig%d" % j, tag="ig")
            nc.vector.tensor_tensor(out=t[:], in0=gate[(j, 0)][:], in1=gate[(j, 1)][:], op=ALU.mult)
            prod[j] = t

        def tr_out(j, what):
            src = gate[(j, 2)] if what == "f" else prod[j]
            bank = back_pool.tile([P, 512], F32, name="ob%s%d" % (what, j), tag="back")
            for t in range(4):
                nc.tensor.transpose(bank[:, t * P:(t + 1) * P], src[:, t * P:(t + 1) * P], ident[:])
            banks[(j, what)] = bank[:].rearrange("p (t h) -> p t h", t=4)

        def cell(j, parts=1):
            m, e = divmod(j, 2)
            if e == 0:
                pair_c[m] = out_pool.tile([P, 4, 256], F32, name="oc%d" % m, tag="oc")
                pair_th[m] = ep_pool.tile([P, 4, 256], F32, name="th%d" % m, tag="th")
            cols = slice(e * P, (e + 1) * P)
            t1 = ep_pool.tile([P, 4, P], F32, name="t1_%d" % j, tag="t1")
            n = 4 // parts
            for part in range(parts):
                ts = slice(part * n, (part + 1) * n)
                nc.vector.tensor_tensor(
                    out=t1[:, ts, :], in0=banks[(j, "f")][:, ts, :], in1=c0_half[j // 4][:, ts, (j % 4) * P:(j % 4 + 1) * P], op=ALU.mult,
                )
                nc.vector.tensor_tensor(
                    out=pair_c[m][:, ts, cols], in0=banks[(j, "u")][:, ts, :], in1=t1[:, ts, :], op=ALU.add,
                )
            if e == 1:
                nc.sync.dma_start(out=out_c[:, :, m * 256:(m + 1) * 256], in_=pair_c[m][:])

        def tanh_cell(j, parts=1):
            m, e = divmod(j, 2)
            cols = slice(e * P, (e + 1) * P)
            n = 4 // parts
            for part in range(parts):
                ts = slice(part * n, (part + 1) * n)
                nc.scalar.activation(out=pair_th[m][:, ts, cols], in_=pair_c[m][:, ts, cols], func=ACT.Tanh)

        def add_bias_o(m, half):
            pair_o[(m, half)] = act_pool.tile([P, 2, 256], F32, name="o%d_%d" % (m, half), tag="o%d" % half)
            nc.vector.tensor_tensor(
                out=pair_o[(m, half)][:], in0=accs[(4 * m + 3, half)],
                in1=bias_o[:, m * 256:(m + 1) * 256].unsqueeze(1).to_broadcast([P, 2, 256]), op=ALU.add,
            )

        def sigmoid_o(m, half):
            o = pair_o[(m, half)]
            nc.scalar.activation(out=o[:], in_=o[:], func=ACT.Sigmoid)

        def hidden(m, half):
            ts = slice(2 * half, 2 * half + 2)
            if half == 0:
                pair_h[m] = out_pool.tile([P, 4, 256], F32, name="oh%d" % m, tag="oh")
            nc.vector.tensor_tensor(
                out=pair_h[m][:, ts, :], in0=pair_o[(m, half)][:], in1=pair_th[m][:, ts, :], op=ALU.mult,
            )
            if half == 1 or m == NM - 1:
                hs = ts if m == NM - 1 else slice(0, 4)
                nc.sync.dma_start(out=out_h[:, hs, m * 256:(m + 1) * 256], in_=pair_h[m][:, hs, :])

        def do_x(s, th, share):
            key = ("x", s, th)
            transpose(key)
            evacuate(key, 0)
            evacuate(key, 1, on_scalar=not share)

        def do_w(key, share=False):
            transpose(key)
            evacuate(key, 0)
            evacuate(key, 1, on_scalar=not share)

        keep_clock(10, "idle_start")
        do_x(0, 0, True)
        keep_clock(1, "idle_a")
        do_x(0, 1, True)
        keep_clock(1, "idle_b")
        do_w((0, 0))
        quant_x(0, 0)
        quant_x(0, 1)
        do_w((1, 0))
        quant((0, 0))
        do_x(1, 0, False)
        quant((1, 0))
        for hh in range(2):
            mx(0, hh, 0)
        do_x(1, 1, False)
        reorder((0, 1), 2)
        do_w((0, 1))
        reorder((1, 1), 2)
        for hh in range(2):
            mx(1, hh, 0)
        quant_x(1, 0)
        quant_x(1, 1)

        bsum = const.tile([P, P], F32, name="bsum")
        nc.vector.tensor_tensor(out=bsum[:], in0=braw[:, 0:P], in1=braw[:, P:2 * P], op=ALU.add)
        do_w((1, 1))
        quant((0, 1))
        reorder((2, 0), 2)
        pb = tr_pool.tile([P, 512], F32, name="pb", tag="tr")
        nc.tensor.transpose(pb[:, 0:P], bsum[:], ident[:])
        bias_sb = const.tile([P, 32], F32, name="bias_sb")
        nc.vector.tensor_copy(out=bias_sb[:], in_=pb[:, 0:32])
        bias_o = const.tile([P, HID], F32, name="bias_o")

        for r in range(NR):
            m, kind = divmod(r, 4)
            a, b = 2 * m, 2 * m + 1
            if r + 2 < NR:
                for s in range(1 if r == 0 else 0, 2):
                    reorder((r + 2, s))
                    if s == 0 and kind == 0 and m > 0:
                        add_bias_o(m - 1, 1)
            if 0 < r < NR - 1:
                for s in range(2):
                    do_w((r + 1, s))
            if kind == 0 and m > 0:
                tr_out(b - 2, "u")
                sigmoid_o(m - 1, 0)
                cell(b - 2)
            elif kind == 1:
                mul_ig(a)
                if m > 0:
                    tanh_cell(b - 2)
            elif kind == 2:
                tr_out(a, "f")
                tr_out(a, "u")
                if m > 0:
                    hidden(m - 1, 0)
                if m == NM - 1:
                    hidden(m - 1, 1)
                cell(a)
                if 0 < m < NM - 1:
                    sigmoid_o(m - 1, 1)
            elif kind == 3:
                tr_out(b, "f")
                mul_ig(b)
                tanh_cell(a)
            if r + 1 < NR:
                for s in range(1 if r == 0 else 0, 2):
                    quant((r + 1, s))
            if kind == 3 and 0 < m < NM - 1:
                hidden(m - 1, 1)
            if kind < 3:
                for hh in range(2):
                    if r > 1:
                        mx(r, hh, 0)
                    mx(r, hh, 1)
                    act(r, hh)
                if r == NR - 3:
                    sigmoid_o(m - 1, 1)
            elif r + 1 < NR:
                for half in range(2):
                    mx_o(r, half)
                add_bias_o(m, 0)
            if r in (2, 6):
                cs = slice(r // 4 * 512, r // 4 * 512 + 512)
                bank = tr_pool.tile([P, 512], F32, name="bo%d" % r, tag="tr")
                nc.tensor.matmul(out=bank[:], lhsT=ones[:], rhs=orow[:, cs], start=True, stop=True)
                nc.vector.tensor_copy(out=bias_o[:, cs], in_=bank[:])
            if r + AHEAD < NR:
                load_round(r + AHEAD)

        m, j = NM - 1, NT - 1
        cols = slice(m * 256, (m + 1) * 256)
        late = slice(P, 2 * P)
        mx_o(NR - 1, 0, tr_pool, "tr")
        tr_out(j, "u")
        mx_o(NR - 1, 1, tr_pool, "tr")
        t1 = ep_pool.tile([P, 4, P], F32, name="t1_%d" % j, tag="t1")
        nc.vector.tensor_tensor(
            out=t1[:], in0=banks[(j, "f")], in1=c0_half[1][:, :, HID // 2 - P:HID // 2], op=ALU.mult,
        )
        add_bias_o(m, 0)
        sigmoid_o(m, 0)
        for half in range(2):
            ts = slice(2 * half, 2 * half + 2)
            nc.vector.tensor_tensor(
                out=pair_c[m][:, ts, late], in0=banks[(j, "u")][:, ts, :], in1=t1[:, ts, :], op=ALU.add,
            )
            nc.scalar.activation(out=pair_th[m][:, ts, late], in_=pair_c[m][:, ts, late], func=ACT.Tanh)
        nc.sync.dma_start(out=out_c[:, :, cols], in_=pair_c[m][:])
        pair_o[(m, 1)] = act_pool.tile([P, 2, 256], F32, name="o%d_1" % m, tag="o1")
        o1 = pair_o[(m, 1)]
        for tt in range(2):
            nc.vector.tensor_tensor(
                out=o1[:, tt, :], in0=accs[(NR - 1, 1)][:, tt, :], in1=bias_o[:, cols], op=ALU.add,
            )
            nc.scalar.activation(out=o1[:, tt, :], in_=o1[:, tt, :], func=ACT.Sigmoid)
        hidden(m, 0)
        for tt in range(2):
            t = 2 + tt
            nc.vector.tensor_tensor(
                out=pair_h[m][:, t, :], in0=o1[:, tt, :], in1=pair_th[m][:, t, :], op=ALU.mult,
            )
            nc.sync.dma_start(out=out_h[:, t, cols], in_=pair_h[m][:, t, :])
